import numpy as np
import ml_dtypes


def mxq(x, axis, fmt="e4m3"):
    dtype, down = {"e4m3": (ml_dtypes.float8_e4m3fn, 7), "e5m2": (ml_dtypes.float8_e5m2, 14)}[fmt]
    v = np.moveaxis(np.asarray(x, np.float32).astype(ml_dtypes.bfloat16).astype(np.float64), axis, -1)
    blocks = v.reshape(v.shape[:-1] + (-1, 32))
    amax = np.abs(blocks).max(-1, keepdims=True)
    byte = np.maximum(np.where(amax > 0, np.frexp(amax)[1] - 1 + 127, 0) - down, 1)
    scale = np.exp2(byte - 127.0)
    codes = (blocks / scale).astype(np.float32).astype(dtype).astype(np.float64)
    return np.moveaxis((codes * scale).reshape(v.shape), -1, axis)


WIDE = False


def mx_kscale(k):
    if not WIDE:
        return np.ones(k)
    levels = np.array([10, -10, 5, -5, 0])
    a = np.random.permutation(np.resize(levels, k // 512 * 4)).reshape(k // 512, 4)
    idx = np.arange(k)
    return np.exp2(a[idx // 512, idx % 128 // 32])


BF16 = ml_dtypes.bfloat16


def bf(x):
    return np.asarray(x, np.float32).astype(BF16)


def f64(x):
    return np.asarray(x).astype(np.float64)


N, D_IN, H0, H1, K = 8192, 512, 512, 256, 20
V = 1.0


def silu(v):
    return v / (1.0 + np.exp(-v))


def setup_inputs():
    s = mx_kscale(D_IN)
    w1 = np.random.standard_normal((D_IN, H0)) / np.sqrt(D_IN)
    b1 = np.random.standard_normal(H0) * 0.2
    w2 = np.random.standard_normal((H0, H1)) * 4.0 / np.sqrt(H0 * H1)
    b2 = np.random.standard_normal(H1) * 0.1
    cent = np.random.standard_normal((K, D_IN)) * 0.9
    x = cent[np.random.randint(0, K, N)] + np.random.standard_normal((N, D_IN)) * 0.44
    hc = silu(np.stack([(c[:, None] * w1).sum(0) for c in cent]) + b1)
    clusters = (hc[:, :, None] * w2[None]).sum(1) + b2 + np.random.standard_normal((K, H1)) * 0.5 / np.sqrt(H1)
    return {"x": bf(x * s), "W1": bf(w1 / s[:, None]), "b1": bf(b1), "W2": bf(w2), "b2": bf(b2), "clusters": bf(clusters)}


def reference(x, W1, b1, W2, b2, clusters):
    h = silu((mxq(f64(x), 1, "e4m3") @ mxq(f64(W1), 0, "e4m3")) + f64(b1))
    z = (mxq(h, 1, "e4m3") @ mxq(f64(W2), 0, "e4m3")) + f64(b2)
    d2 = np.stack([((z - c) ** 2).sum(1) for c in f64(clusters)], axis=1)
    q = 1.0 / (1.0 + d2 / V)
    q = q ** ((V + 1.0) / 2.0)
    q = q / q.sum(1, keepdims=True)
    return z, q

@@ -1,0 +1,298 @@
+from contextlib import ExitStack
+
+from concourse import mybir
+from concourse.masks import make_identity
+
+F32 = mybir.dt.float32
+BF16 = mybir.dt.bfloat16
+U32 = mybir.dt.uint32
+U8 = mybir.dt.uint8
+FP8X4 = mybir.dt.float8_e4m3fn_x4
+ACT = mybir.ActivationFunctionType
+ALU = mybir.AluOpType
+AX = mybir.AxisListType
+
+P = 128
+N_ROWS, D_IN, H0, H1, KC = 8192, 512, 512, 256, 20
+NB = N_ROWS // P
+TB = 4
+NT = NB // TB
+W = TB * P
+T1_FIRST = 0
+BATCH_ENDS = [3, 7, 11, 13, 14, 15]
+
+FLOPS = 2 * N_ROWS * (D_IN * H0 + H0 * H1 + H1 * KC)
+
+
+def tile_lintrans_pa_t_kernel(tc, x, W1, b1, W2, b2, clusters, out_0, out_1):
+    nc = tc.nc
+    x_v = x.rearrange("(p b) k -> p b k", b=NB)
+    z_v = out_0.rearrange("(p b) j -> p b j", b=NB)
+    q_v = out_1.rearrange("(p b) k -> p b k", b=NB)
+
+    with ExitStack() as es:
+        es.enter_context(tc.manual_schedule())
+        keep = es.enter_context(tc.tile_pool(name="keep", bufs=1))
+        xin_pool = es.enter_context(tc.tile_pool(name="xin", bufs=NT))
+        work = es.enter_context(tc.tile_pool(name="work", bufs=2))
+        work3 = es.enter_context(tc.tile_pool(name="work3", bufs=3))
+        zpool = es.enter_context(tc.tile_pool(name="zpool", bufs=4))
+        psum = es.enter_context(tc.psum_pool(name="psum", bufs=1))
+        n_banks = [0]
+
+        def bank(shape):
+            k = n_banks[0] % 8
+            n_banks[0] += 1
+            return psum.tile(shape, F32, tag="bank%d" % k, name="bank%d" % k)
+
+        ident = keep.tile([P, P], F32)
+        make_identity(nc, ident[:])
+
+        xin = []
+
+        def load_x(i):
+            t = xin_pool.tile([P, TB, D_IN], BF16, name="xin")
+            nc.sync.dma_start(out=t[:], in_=x_v[:, TB * i:TB * (i + 1), :])
+            xin.append(t)
+
+        load_x(0)
+        w1raw = keep.tile([P, 4, H0], BF16)
+        for u in range(2):
+            nc.sync.dma_start(
+                out=w1raw[:, 2 * u:2 * u + 2, :],
+                in_=W1[256 * u:256 * (u + 1), :].rearrange("(q e) c -> q e c", e=2),
+            )
+        b1raw = keep.tile([P, 4], BF16)
+        nc.scalar.dma_start(out=b1raw[:], in_=b1.rearrange("(p m) -> p m", m=4))
+        w2raw = keep.tile([P, 4, H1], BF16)
+        nc.scalar.dma_start(out=w2raw[:], in_=W2.rearrange("(p m) j -> p m j", m=4))
+        par = keep.tile([P, P], BF16)
+        nc.vector.memset(par[:], 0.0)
+        nc.scalar.dma_start(out=par[0:KC, :], in_=clusters[:, 0:P])
+        nc.scalar.dma_start(out=par[32:32 + KC, :], in_=clusters[:, P:2 * P])
+        nc.scalar.dma_start(out=par[64:66, :], in_=b2.rearrange("(h j) -> h j", j=P))
+        b2bc = keep.tile([P, H1], BF16)
+        nc.scalar.dma_start(out=b2bc[:], in_=b2.partition_broadcast(P))
+        for i in range(1, NT):
+            load_x(i)
+
+        ones = keep.tile([P, P], F32)
+        nc.vector.memset(ones[:], 1.0)
+
+        w1g = keep.tile([P, H0, 4], BF16, align_bytes=64)
+        w1q = keep.tile([P, H0], U32, align_bytes=64)
+        w1s = keep.tile([P, H0], U8, align_bytes=64)
+        b1col = keep.tile([P, 4], F32)
+        w2g = keep.tile([P, H1, 4], BF16, align_bytes=64)
+        w2q = keep.tile([P, H1], U32, align_bytes=64)
+        w2s = keep.tile([P, H1], U8, align_bytes=64)
+        m2cT = keep.tile([P, 2, KC], F32)
+        e_bc = keep.tile([P, KC], F32)
+        ssq = keep.tile([P, NB], F32)
+        den = keep.tile([P, NB, KC], F32)
+        rsum = keep.tile([P, NB], F32)
+
+        def setup_w1():
+            nc.vector.tensor_copy(
+                out=w1g[:].rearrange("q (m p) t -> q m p t", m=4),
+                in_=w1raw[:].rearrange("q t (p m) -> q m p t", m=4),
+            )
+            nc.vector.tensor_copy(out=b1col[:], in_=b1raw[:])
+            nc.vector.quantize_mx(out=w1q[:].bitcast(FP8X4), scales=w1s[:],
+                                  in_=w1g[:].rearrange("q c t -> q (c t)"))
+
+        def setup_w2():
+            nc.vector.tensor_copy(out=w2g[:], in_=w2raw[:].rearrange("p m j -> p j m"))
+
+        def setup_w2q():
+            nc.vector.quantize_mx(out=w2q[:].bitcast(FP8X4), scales=w2s[:],
+                                  in_=w2g[:].rearrange("p j m -> p (j m)"))
+
+        def setup_consts():
+            parf = keep.tile([P, P], F32)
+            nc.vector.tensor_copy(out=parf[:], in_=par[:])
+            par_ps = bank([P, P])
+            nc.tensor.transpose(par_ps[:], parf[:], ident[:])
+            cst = keep.tile([P, P], F32)
+            nc.vector.tensor_copy(out=cst[:], in_=par_ps[:])
+            cT = cst[:, 0:64].rearrange("p (h k) -> p h k", h=2)[:, :, 0:KC]
+            nc.vector.tensor_scalar(out=m2cT[:], in0=cT, scalar1=-2.0, scalar2=None, op0=ALU.mult)
+            b2x2 = keep.tile([P, 2], F32)
+            nc.vector.tensor_scalar(out=b2x2[:], in0=cst[:, 64:66], scalar1=2.0, scalar2=None, op0=ALU.mult)
+            cw = keep.tile([P, 2, KC], F32)
+            for h in range(2):
+                nc.vector.tensor_scalar(out=cw[:, h, :], in0=cT[:, h, :], scalar1=b2x2[:, h:h + 1],
+                                        scalar2=None, op0=ALU.subtract)
+            nc.vector.tensor_tensor(out=cw[:], in0=cw[:], in1=cT, op=ALU.mult)
+            e_ps = bank([P, KC])
+            for h in range(2):
+                nc.tensor.matmul(e_ps[:], lhsT=ones[:], rhs=cw[:, h, :], start=(h == 0), stop=(h == 1))
+            nc.vector.tensor_scalar(out=e_bc[:], in0=e_ps[:], scalar1=1.0, scalar2=None, op0=ALU.add)
+
+        st = {}
+
+        def ok(i):
+            return 0 <= i < NT
+
+        def fA(i):
+            xf = xin[i][:].bitcast(F32)
+            for pr in range(2):
+                xt = bank([P, 2, 2, P])
+                st[("xt", i, pr)] = xt
+                for bb in range(2):
+                    for u in range(2):
+                        nc.tensor.transpose(xt[:, bb, u, :], xf[:, 2 * pr + bb, P * u:P * (u + 1)], ident[:])
+
+        def fT1(i, pr):
+            if pr == T1_FIRST:
+                xg = work.tile([P, W * 4], BF16, align_bytes=64, name="xg")
+                st[("xg", i)] = xg
+            xg = st[("xg", i)]
+            xgf = xg[:].bitcast(F32).rearrange("p (b n u) -> p b n u", b=TB, u=2)
+            src = st[("xt", i, pr)][:].rearrange("p b u n -> p b n u")
+            if pr == 1:
+                nc.scalar.copy(out=xgf[:, 2:4, :, :], in_=src)
+            else:
+                nc.vector.tensor_copy(out=xgf[:, 0:2, :, :], in_=src)
+
+        def fT2(i):
+            xq = work3.tile([P, W], U32, align_bytes=64, name="xq")
+            xs = work3.tile([P, W], U8, align_bytes=64, name="xs")
+            st[("xq", i)] = (xq, xs)
+            nc.vector.quantize_mx(out=xq[:].bitcast(FP8X4), scales=xs[:], in_=st[("xg", i)][:])
+
+        def fB(i, m):
+            xq, xs = st[("xq", i)]
+            hp = bank([P, W])
+            st[("hp", i, m)] = hp
+            nc.tensor.matmul_mx(out=hp[:], lhsT=w1q[:, P * m:P * (m + 1)].bitcast(FP8X4),
+                                lhsT_scale=w1s[:, P * m:P * (m + 1)],
+                                rhs=xq[:].bitcast(FP8X4), rhs_scale=xs[:], start=True, stop=True)
+
+        def fT3(i, m):
+            if m == 0:
+                st[("hb", i)] = work.tile([P, 4, W], BF16, name="hb")
+            nc.scalar.activation(out=st[("hb", i)][:, m, :], in_=st[("hp", i, m)][:], func=ACT.Silu,
+                                 bias=b1col[:, m:m + 1], scale=1.0)
+
+        def fT4(i):
+            hg = work.tile([P, W, 4], BF16, align_bytes=64, name="hg")
+            st[("hg", i)] = hg
+            nc.vector.tensor_copy(out=hg[:].rearrange("p (c i) t -> p c t i", i=4),
+                                  in_=st[("hb", i)][:].rearrange("p t (c i) -> p c t i", i=4))
+
+        def fT5(i):
+            hq = work.tile([P, W], U32, align_bytes=64, name="hq")
+            hs = work.tile([P, W], U8, align_bytes=64, name="hs")
+            st[("hq", i)] = (hq, hs)
+            nc.vector.quantize_mx(out=hq[:].bitcast(FP8X4), scales=hs[:],
+                                  in_=st[("hg", i)][:].rearrange("p n t -> p (n t)"))
+
+        def fC(i, pr):
+            hq, hs = st[("hq", i)]
+            up = bank([P, 2, H1])
+            st[("up", i, pr)] = up
+            for bb in range(2):
+                blk = 2 * pr + bb
+                nc.tensor.matmul_mx(out=up[:, bb, :], lhsT=hq[:, P * blk:P * (blk + 1)].bitcast(FP8X4),
+                                    lhsT_scale=hs[:, P * blk:P * (blk + 1)],
+                                    rhs=w2q[:].bitcast(FP8X4), rhs_scale=w2s[:], start=True, stop=True)
+
+        def fD(i, h):
+            hq, hs = st[("hq", i)]
+            ut = bank([P, W])
+            st[("ut", i, h)] = ut
+            nc.tensor.matmul_mx(out=ut[:], lhsT=w2q[:, P * h:P * (h + 1)].bitcast(FP8X4),
+                                lhsT_scale=w2s[:, P * h:P * (h + 1)],
+                                rhs=hq[:].bitcast(FP8X4), rhs_scale=hs[:], start=True, stop=True)
+
+        def fT6(i, pr):
+            if pr == 0:
+                st[("z", i)] = zpool.tile([P, TB, H1], F32, name="zsb")
+            nc.vector.tensor_tensor(out=st[("z", i)][:, 2 * pr:2 * pr + 2, :], in0=st[("up", i, pr)][:],
+                                    in1=b2bc[:].unsqueeze(1).to_broadcast([P, 2, H1]), op=ALU.add)
+            if pr == 1:
+                nc.sync.dma_start(out=z_v[:, TB * i:TB * (i + 1), :], in_=st[("z", i)][:])
+
+        def fT7(i, h):
+            if h == 0:
+                st[("uT", i)] = work.tile([P, 2, W], F32, name="uT")
+            nc.scalar.copy(out=st[("uT", i)][:, h, :], in_=st[("ut", i, h)][:])
+
+        def fT8(i):
+            for blk in range(TB):
+                junk = work.tile([P, H1], BF16, name="junk")
+                nc.scalar.activation(out=junk[:], in_=st[("z", i)][:, blk, :], func=ACT.Square,
+                                     accum_out=ssq[:, TB * i + blk:TB * i + blk + 1])
+
+        def fE(i):
+            uT = st[("uT", i)]
+            dp = bank([P, TB, KC])
+            st[("dp", i)] = dp
+            for blk in range(TB):
+                for h in range(2):
+                    nc.tensor.matmul(dp[:, blk, :], lhsT=uT[:, h, P * blk:P * (blk + 1)], rhs=m2cT[:, h, :],
+                                     start=(h == 0), stop=(h == 1))
+
+        def fT9(i):
+            d = den[:, TB * i:TB * (i + 1), :]
+            nc.vector.tensor_tensor(out=d, in0=st[("dp", i)][:],
+                                    in1=e_bc[:].unsqueeze(1).to_broadcast([P, TB, KC]), op=ALU.add)
+            nc.vector.tensor_tensor(out=d, in0=d,
+                                    in1=ssq[:, TB * i:TB * (i + 1)].unsqueeze(2).to_broadcast([P, TB, KC]),
+                                    op=ALU.add)
+            nc.vector.reciprocal(out=d, in_=d)
+
+        def finish(b0, b9):
+            nb = b9 - b0
+            d = den[:, b0:b9, :]
+            nc.vector.tensor_reduce(out=rsum[:, b0:b9], in_=d, axis=AX.X, op=ALU.add)
+            nc.vector.reciprocal(out=rsum[:, b0:b9], in_=rsum[:, b0:b9])
+            nc.vector.tensor_tensor(out=d, in0=d, in1=rsum[:, b0:b9].unsqueeze(2).to_broadcast([P, nb, KC]),
+                                    op=ALU.mult)
+            nc.sync.dma_start(out=q_v[:, b0:b9, :], in_=d)
+
+        setup_w1()
+        first = [0]
+        for p in range(NT + 6):
+            if ok(p - 3):
+                fT4(p - 3)
+            if ok(p - 2):
+                for m in range(4):
+                    fB(p - 2, m)
+                for m in range(4):
+                    fT3(p - 2, m)
+            if ok(p - 1):
+                fT2(p - 1)
+            if p == 1:
+                setup_w2()
+            if ok(p - 4):
+                fC(p - 4, 0)
+                fD(p - 4, 0)
+                fC(p - 4, 1)
+                fD(p - 4, 1)
+            if ok(p - 3):
+                fT5(p - 3)
+            if ok(p - 4):
+                fT6(p - 4, 0)
+                fT6(p - 4, 1)
+            if ok(p - 5):
+                fE(p - 5)
+            if ok(p - 4):
+                fT7(p - 4, 0)
+                fT7(p - 4, 1)
+            if p == 2:
+                setup_w2q()
+                setup_consts()
+            if ok(p):
+                fA(p)
+            if ok(p - 5):
+                fT9(p - 5)
+                if (p - 5) in BATCH_ENDS:
+                    finish(TB * first[0], TB * (p - 4))
+                    first[0] = p - 4
+            if ok(p - 4):
+                fT8(p - 4)
+            if ok(p):
+                fT1(p, 0)
+                fT1(p, 1)

@@ -31,19 +31,18 @@ def tile_lintrans_pa_t_kernel(tc, x, W1, b1, W2, b2, clusters, out_0, out_1):
     q_v = out_1.rearrange("(p b) k -> p b k", b=NB)
 
     with ExitStack() as es:
-        es.enter_context(tc.manual_schedule())
         keep = es.enter_context(tc.tile_pool(name="keep", bufs=1))
         xin_pool = es.enter_context(tc.tile_pool(name="xin", bufs=NT))
         work = es.enter_context(tc.tile_pool(name="work", bufs=2))
         work3 = es.enter_context(tc.tile_pool(name="work3", bufs=3))
         zpool = es.enter_context(tc.tile_pool(name="zpool", bufs=4))
-        psum = es.enter_context(tc.psum_pool(name="psum", bufs=1))
+        psum = es.enter_context(tc.psum_pool(name="psum", bufs=8))
         n_banks = [0]
 
         def bank(shape):
             k = n_banks[0] % 8
             n_banks[0] += 1
-            return psum.tile(shape, F32, tag="bank%d" % k, name="bank%d" % k)
+            return psum.tile(shape, F32, tag="bank", name="bank")
 
         ident = keep.tile([P, P], F32)
         make_identity(nc, ident[:])
@@ -86,7 +85,7 @@ def tile_lintrans_pa_t_kernel(tc, x, W1, b1, W2, b2, clusters, out_0, out_1):
         w2g = keep.tile([P, H1, 4], BF16, align_bytes=64)
         w2q = keep.tile([P, H1], U32, align_bytes=64)
         w2s = keep.tile([P, H1], U8, align_bytes=64)
-        m2cT = keep.tile([P, 2, KC], F32)
+        m2cT = keep.tile([P, 2, KC], BF16)
         e_bc = keep.tile([P, KC], F32)
         ssq = keep.tile([P, NB], F32)
         den = keep.tile([P, NB, KC], F32)
@@ -150,10 +149,7 @@ def tile_lintrans_pa_t_kernel(tc, x, W1, b1, W2, b2, clusters, out_0, out_1):
             xg = st[("xg", i)]
             xgf = xg[:].bitcast(F32).rearrange("p (b n u) -> p b n u", b=TB, u=2)
             src = st[("xt", i, pr)][:].rearrange("p b u n -> p b n u")
-            if pr == 1:
-                nc.scalar.copy(out=xgf[:, 2:4, :, :], in_=src)
-            else:
-                nc.vector.tensor_copy(out=xgf[:, 0:2, :, :], in_=src)
+            nc.scalar.copy(out=xgf[:, 2 * pr:2 * pr + 2, :, :], in_=src)
 
         def fT2(i):
             xq = work3.tile([P, W], U32, align_bytes=64, name="xq")
@@ -216,8 +212,14 @@ def tile_lintrans_pa_t_kernel(tc, x, W1, b1, W2, b2, clusters, out_0, out_1):
 
         def fT7(i, h):
             if h == 0:
-                st[("uT", i)] = work.tile([P, 2, W], F32, name="uT")
-            nc.scalar.copy(out=st[("uT", i)][:, h, :], in_=st[("ut", i, h)][:])
+                st[("uh", i)] = work.tile([P, 2, W], BF16, name="uh")
+            nc.scalar.copy(out=st[("uh", i)][:, h, :], in_=st[("ut", i, h)][:])
+
+        def fT7lo(i, h):
+            if h == 0:
+                st[("ul", i)] = work.tile([P, 2, W], BF16, name="ul")
+            nc.vector.tensor_tensor(out=st[("ul", i)][:, h, :], in0=st[("ut", i, h)][:],
+                                    in1=st[("uh", i)][:, h, :], op=ALU.subtract)
 
         def fT8(i):
             for blk in range(TB):
@@ -226,13 +228,14 @@ def tile_lintrans_pa_t_kernel(tc, x, W1, b1, W2, b2, clusters, out_0, out_1):
                                      accum_out=ssq[:, TB * i + blk:TB * i + blk + 1])
 
         def fE(i):
-            uT = st[("uT", i)]
+            parts = (st[("uh", i)], st[("ul", i)])
             dp = bank([P, TB, KC])
             st[("dp", i)] = dp
             for blk in range(TB):
-                for h in range(2):
-                    nc.tensor.matmul(dp[:, blk, :], lhsT=uT[:, h, P * blk:P * (blk + 1)], rhs=m2cT[:, h, :],
-                                     start=(h == 0), stop=(h == 1))
+                for n in range(4):
+                    h = n // 2
+                    nc.tensor.matmul(dp[:, blk, :], lhsT=parts[n % 2][:, h, P * blk:P * (blk + 1)],
+                                     rhs=m2cT[:, h, :], start=(n == 0), stop=(n == 3))
 
         def fT9(i):
             d = den[:, TB * i:TB * (i + 1), :]
@@ -281,6 +284,8 @@ def tile_lintrans_pa_t_kernel(tc, x, W1, b1, W2, b2, clusters, out_0, out_1):
             if ok(p - 4):
                 fT7(p - 4, 0)
                 fT7(p - 4, 1)
+                fT7lo(p - 4, 0)
+                fT7lo(p - 4, 1)
             if p == 2:
                 setup_w2q()
                 setup_consts()

@@ -174,8 +174,11 @@ def tile_lintrans_pa_t_kernel(tc, x, W1, b1, W2, b2, clusters, out_0, out_1):
         def fT4(i):
             hg = work.tile([P, W, 4], BF16, align_bytes=64, name="hg")
             st[("hg", i)] = hg
-            nc.vector.tensor_copy(out=hg[:].rearrange("p (c i) t -> p c t i", i=4),
-                                  in_=st[("hb", i)][:].rearrange("p t (c i) -> p c t i", i=4))
+            for c in range(2):
+                cols = slice(c * (W // 2), (c + 1) * (W // 2))
+                nc.gpsimd.tensor_scalar(out=hg[:, cols, :],
+                                        in0=st[("hb", i)][:, :, cols].rearrange("p t n -> p n t"),
+                                        scalar1=1.0, scalar2=0.0, op0=ALU.mult, op1=ALU.add)
 
         def fT5(i):
             hq = work.tile([P, W], U32, align_bytes=64, name="hq")

@@ -19,6 +19,8 @@ TB = 4
 NT = NB // TB
 W = TB * P
 T1_FIRST = 0
+F32_TILES = []
+T1_ON_VECTOR = [0, 2, 4, 6, 8, 10, 12, 14]
 BATCH_ENDS = [3, 7, 11, 13, 14, 15]
 
 FLOPS = 2 * N_ROWS * (D_IN * H0 + H0 * H1 + H1 * KC)
@@ -86,6 +88,7 @@ def tile_lintrans_pa_t_kernel(tc, x, W1, b1, W2, b2, clusters, out_0, out_1):
         w2q = keep.tile([P, H1], U32, align_bytes=64)
         w2s = keep.tile([P, H1], U8, align_bytes=64)
         m2cT = keep.tile([P, 2, KC], BF16)
+        m2cF = keep.tile([P, 2, KC], F32)
         e_bc = keep.tile([P, KC], F32)
         ssq = keep.tile([P, NB], F32)
         den = keep.tile([P, NB, KC], F32)
@@ -116,6 +119,7 @@ def tile_lintrans_pa_t_kernel(tc, x, W1, b1, W2, b2, clusters, out_0, out_1):
             nc.vector.tensor_copy(out=cst[:], in_=par_ps[:])
             cT = cst[:, 0:64].rearrange("p (h k) -> p h k", h=2)[:, :, 0:KC]
             nc.vector.tensor_scalar(out=m2cT[:], in0=cT, scalar1=-2.0, scalar2=None, op0=ALU.mult)
+            nc.vector.tensor_scalar(out=m2cF[:], in0=cT, scalar1=-2.0, scalar2=None, op0=ALU.mult)
             b2x2 = keep.tile([P, 2], F32)
             nc.vector.tensor_scalar(out=b2x2[:], in0=cst[:, 64:66], scalar1=2.0, scalar2=None, op0=ALU.mult)
             cw = keep.tile([P, 2, KC], F32)
@@ -149,7 +153,10 @@ def tile_lintrans_pa_t_kernel(tc, x, W1, b1, W2, b2, clusters, out_0, out_1):
             xg = st[("xg", i)]
             xgf = xg[:].bitcast(F32).rearrange("p (b n u) -> p b n u", b=TB, u=2)
             src = st[("xt", i, pr)][:].rearrange("p b u n -> p b n u")
-            nc.scalar.copy(out=xgf[:, 2 * pr:2 * pr + 2, :, :], in_=src)
+            if pr == 0 and i in T1_ON_VECTOR:
+                nc.vector.tensor_copy(out=xgf[:, 2 * pr:2 * pr + 2, :, :], in_=src)
+            else:
+                nc.scalar.copy(out=xgf[:, 2 * pr:2 * pr + 2, :, :], in_=src)
 
         def fT2(i):
             xq = work3.tile([P, W], U32, align_bytes=64, name="xq")
@@ -174,11 +181,8 @@ def tile_lintrans_pa_t_kernel(tc, x, W1, b1, W2, b2, clusters, out_0, out_1):
         def fT4(i):
             hg = work.tile([P, W, 4], BF16, align_bytes=64, name="hg")
             st[("hg", i)] = hg
-            for c in range(2):
-                cols = slice(c * (W // 2), (c + 1) * (W // 2))
-                nc.gpsimd.tensor_scalar(out=hg[:, cols, :],
-                                        in0=st[("hb", i)][:, :, cols].rearrange("p t n -> p n t"),
-                                        scalar1=1.0, scalar2=0.0, op0=ALU.mult, op1=ALU.add)
+            nc.vector.tensor_copy(out=hg[:].rearrange("p (c i) t -> p c t i", i=4),
+                                  in_=st[("hb", i)][:].rearrange("p t (c i) -> p c t i", i=4))
 
         def fT5(i):
             hq = work.tile([P, W], U32, align_bytes=64, name="hq")
@@ -214,11 +218,20 @@ def tile_lintrans_pa_t_kernel(tc, x, W1, b1, W2, b2, clusters, out_0, out_1):
                 nc.sync.dma_start(out=z_v[:, TB * i:TB * (i + 1), :], in_=st[("z", i)][:])
 
         def fT7(i, h):
+            if i in F32_TILES:
+                if h == 0:
+                    st[("uf", i)] = work.tile([P, 2, W], F32, name="uf")
+                    nc.scalar.copy(out=st[("uf", i)][:, h, :], in_=st[("ut", i, h)][:])
+                else:
+                    nc.vector.tensor_copy(out=st[("uf", i)][:, h, :], in_=st[("ut", i, h)][:])
+                return
             if h == 0:
                 st[("uh", i)] = work.tile([P, 2, W], BF16, name="uh")
             nc.scalar.copy(out=st[("uh", i)][:, h, :], in_=st[("ut", i, h)][:])
 
         def fT7lo(i, h):
+            if i in F32_TILES:
+                return
             if h == 0:
                 st[("ul", i)] = work.tile([P, 2, W], BF16, name="ul")
             nc.vector.tensor_tensor(out=st[("ul", i)][:, h, :], in0=st[("ut", i, h)][:],
@@ -231,9 +244,15 @@ def tile_lintrans_pa_t_kernel(tc, x, W1, b1, W2, b2, clusters, out_0, out_1):
                                      accum_out=ssq[:, TB * i + blk:TB * i + blk + 1])
 
         def fE(i):
-            parts = (st[("uh", i)], st[("ul", i)])
             dp = bank([P, TB, KC])
             st[("dp", i)] = dp
+            if i in F32_TILES:
+                for blk in range(TB):
+                    for h in range(2):
+                        nc.tensor.matmul(dp[:, blk, :], lhsT=st[("uf", i)][:, h, P * blk:P * (blk + 1)],
+                                         rhs=m2cF[:, h, :], start=(h == 0), stop=(h == 1))
+                return
+            parts = (st[("uh", i)], st[("ul", i)])
             for blk in range(TB):
                 for n in range(4):
                     h = n // 2

@@ -19,8 +19,8 @@ TB = 4
 NT = NB // TB
 W = TB * P
 T1_FIRST = 0
-F32_TILES = []
-T1_ON_VECTOR = [0, 2, 4, 6, 8, 10, 12, 14]
+DLAG = 4
+T1_ON_VECTOR = [2, 6, 10, 14]
 BATCH_ENDS = [3, 7, 11, 13, 14, 15]
 
 FLOPS = 2 * N_ROWS * (D_IN * H0 + H0 * H1 + H1 * KC)
@@ -35,9 +35,10 @@ def tile_lintrans_pa_t_kernel(tc, x, W1, b1, W2, b2, clusters, out_0, out_1):
     with ExitStack() as es:
         keep = es.enter_context(tc.tile_pool(name="keep", bufs=1))
         xin_pool = es.enter_context(tc.tile_pool(name="xin", bufs=NT))
-        work = es.enter_context(tc.tile_pool(name="work", bufs=2))
+        work = es.enter_context(tc.tile_pool(name="work", bufs=3))
         work3 = es.enter_context(tc.tile_pool(name="work3", bufs=3))
-        zpool = es.enter_context(tc.tile_pool(name="zpool", bufs=4))
+        zpool = es.enter_context(tc.tile_pool(name="zpool", bufs=DLAG + 4))
+        hqpool = es.enter_context(tc.tile_pool(name="hqpool", bufs=DLAG + 3))
         psum = es.enter_context(tc.psum_pool(name="psum", bufs=8))
         n_banks = [0]
 
@@ -88,8 +89,9 @@ def tile_lintrans_pa_t_kernel(tc, x, W1, b1, W2, b2, clusters, out_0, out_1):
         w2q = keep.tile([P, H1], U32, align_bytes=64)
         w2s = keep.tile([P, H1], U8, align_bytes=64)
         m2cT = keep.tile([P, 2, KC], BF16)
-        m2cF = keep.tile([P, 2, KC], F32)
         e_bc = keep.tile([P, KC], F32)
+        e_rows = keep.tile([P, KC], BF16)
+        pick = keep.tile([P, 1], BF16)
         ssq = keep.tile([P, NB], F32)
         den = keep.tile([P, NB, KC], F32)
         rsum = keep.tile([P, NB], F32)
@@ -119,7 +121,6 @@ def tile_lintrans_pa_t_kernel(tc, x, W1, b1, W2, b2, clusters, out_0, out_1):
             nc.vector.tensor_copy(out=cst[:], in_=par_ps[:])
             cT = cst[:, 0:64].rearrange("p (h k) -> p h k", h=2)[:, :, 0:KC]
             nc.vector.tensor_scalar(out=m2cT[:], in0=cT, scalar1=-2.0, scalar2=None, op0=ALU.mult)
-            nc.vector.tensor_scalar(out=m2cF[:], in0=cT, scalar1=-2.0, scalar2=None, op0=ALU.mult)
             b2x2 = keep.tile([P, 2], F32)
             nc.vector.tensor_scalar(out=b2x2[:], in0=cst[:, 64:66], scalar1=2.0, scalar2=None, op0=ALU.mult)
             cw = keep.tile([P, 2, KC], F32)
@@ -131,6 +132,16 @@ def tile_lintrans_pa_t_kernel(tc, x, W1, b1, W2, b2, clusters, out_0, out_1):
             for h in range(2):
                 nc.tensor.matmul(e_ps[:], lhsT=ones[:], rhs=cw[:, h, :], start=(h == 0), stop=(h == 1))
             nc.vector.tensor_scalar(out=e_bc[:], in0=e_ps[:], scalar1=1.0, scalar2=None, op0=ALU.add)
+            term = keep.tile([P, 3, KC], BF16)
+            for g in range(3):
+                nc.vector.tensor_copy(out=term[:, g, :], in_=e_bc[:])
+                nc.vector.tensor_tensor(out=e_bc[:], in0=e_bc[:], in1=term[:, g, :], op=ALU.subtract)
+            nc.vector.memset(e_rows[:], 0.0)
+            for g in range(3):
+                rows = slice(32 * g, 32 * (g + 1))
+                nc.vector.tensor_copy(out=e_rows[rows, :], in_=term[rows, g, :])
+            nc.vector.tensor_tensor(out=pick[:], in0=ident[:, 0:1], in1=ident[:, 32:33], op=ALU.add)
+            nc.vector.tensor_tensor(out=pick[:], in0=pick[:], in1=ident[:, 64:65], op=ALU.add)
 
         st = {}
 
@@ -185,8 +196,8 @@ def tile_lintrans_pa_t_kernel(tc, x, W1, b1, W2, b2, clusters, out_0, out_1):
                                   in_=st[("hb", i)][:].rearrange("p t (c i) -> p c t i", i=4))
 
         def fT5(i):
-            hq = work.tile([P, W], U32, align_bytes=64, name="hq")
-            hs = work.tile([P, W], U8, align_bytes=64, name="hs")
+            hq = hqpool.tile([P, W], U32, align_bytes=64, name="hq")
+            hs = hqpool.tile([P, W], U8, align_bytes=64, name="hs")
             st[("hq", i)] = (hq, hs)
             nc.vector.quantize_mx(out=hq[:].bitcast(FP8X4), scales=hs[:],
                                   in_=st[("hg", i)][:].rearrange("p n t -> p (n t)"))
@@ -218,20 +229,11 @@ def tile_lintrans_pa_t_kernel(tc, x, W1, b1, W2, b2, clusters, out_0, out_1):
                 nc.sync.dma_start(out=z_v[:, TB * i:TB * (i + 1), :], in_=st[("z", i)][:])
 
         def fT7(i, h):
-            if i in F32_TILES:
-                if h == 0:
-                    st[("uf", i)] = work.tile([P, 2, W], F32, name="uf")
-                    nc.scalar.copy(out=st[("uf", i)][:, h, :], in_=st[("ut", i, h)][:])
-                else:
-                    nc.vector.tensor_copy(out=st[("uf", i)][:, h, :], in_=st[("ut", i, h)][:])
-                return
             if h == 0:
                 st[("uh", i)] = work.tile([P, 2, W], BF16, name="uh")
             nc.scalar.copy(out=st[("uh", i)][:, h, :], in_=st[("ut", i, h)][:])
 
         def fT7lo(i, h):
-            if i in F32_TILES:
-                return
             if h == 0:
                 st[("ul", i)] = work.tile([P, 2, W], BF16, name="ul")
             nc.vector.tensor_tensor(out=st[("ul", i)][:, h, :], in0=st[("ut", i, h)][:],
@@ -246,24 +248,18 @@ def tile_lintrans_pa_t_kernel(tc, x, W1, b1, W2, b2, clusters, out_0, out_1):
         def fE(i):
             dp = bank([P, TB, KC])
             st[("dp", i)] = dp
-            if i in F32_TILES:
-                for blk in range(TB):
-                    for h in range(2):
-                        nc.tensor.matmul(dp[:, blk, :], lhsT=st[("uf", i)][:, h, P * blk:P * (blk + 1)],
-                                         rhs=m2cF[:, h, :], start=(h == 0), stop=(h == 1))
-                return
             parts = (st[("uh", i)], st[("ul", i)])
             for blk in range(TB):
                 for n in range(4):
                     h = n // 2
                     nc.tensor.matmul(dp[:, blk, :], lhsT=parts[n % 2][:, h, P * blk:P * (blk + 1)],
-                                     rhs=m2cT[:, h, :], start=(n == 0), stop=(n == 3))
+                                     rhs=m2cT[:, h, :], start=(n == 0), stop=False)
+                nc.tensor.matmul(dp[:, blk, :], lhsT=pick[:].to_broadcast([P, P]), rhs=e_rows[:],
+                                 start=False, stop=True)
 
         def fT9(i):
             d = den[:, TB * i:TB * (i + 1), :]
             nc.vector.tensor_tensor(out=d, in0=st[("dp", i)][:],
-                                    in1=e_bc[:].unsqueeze(1).to_broadcast([P, TB, KC]), op=ALU.add)
-            nc.vector.tensor_tensor(out=d, in0=d,
                                     in1=ssq[:, TB * i:TB * (i + 1)].unsqueeze(2).to_broadcast([P, TB, KC]),
                                     op=ALU.add)
             nc.vector.reciprocal(out=d, in_=d)
@@ -279,7 +275,8 @@ def tile_lintrans_pa_t_kernel(tc, x, W1, b1, W2, b2, clusters, out_0, out_1):
 
         setup_w1()
         first = [0]
-        for p in range(NT + 6):
+        for p in range(NT + 6 + DLAG):
+            d = p - 4 - DLAG
             if ok(p - 3):
                 fT4(p - 3)
             if ok(p - 2):
@@ -293,33 +290,34 @@ def tile_lintrans_pa_t_kernel(tc, x, W1, b1, W2, b2, clusters, out_0, out_1):
                 setup_w2()
             if ok(p - 4):
                 fC(p - 4, 0)
-                fD(p - 4, 0)
                 fC(p - 4, 1)
-                fD(p - 4, 1)
+            if ok(d):
+                fD(d, 0)
+                fD(d, 1)
             if ok(p - 3):
                 fT5(p - 3)
             if ok(p - 4):
                 fT6(p - 4, 0)
                 fT6(p - 4, 1)
-            if ok(p - 5):
-                fE(p - 5)
-            if ok(p - 4):
-                fT7(p - 4, 0)
-                fT7(p - 4, 1)
-                fT7lo(p - 4, 0)
-                fT7lo(p - 4, 1)
+            if ok(d - 1):
+                fE(d - 1)
+            if ok(d):
+                fT7(d, 0)
+                fT7(d, 1)
+                fT7lo(d, 0)
+                fT7lo(d, 1)
             if p == 2:
                 setup_w2q()
                 setup_consts()
             if ok(p):
                 fA(p)
-            if ok(p - 5):
-                fT9(p - 5)
-                if (p - 5) in BATCH_ENDS:
-                    finish(TB * first[0], TB * (p - 4))
-                    first[0] = p - 4
-            if ok(p - 4):
-                fT8(p - 4)
+            if ok(d - 1):
+                fT9(d - 1)
+                if (d - 1) in BATCH_ENDS:
+                    finish(TB * first[0], TB * d)
+                    first[0] = d
+            if ok(d):
+                fT8(d)
             if ok(p):
                 fT1(p, 0)
                 fT1(p, 1)

@@ -18,10 +18,12 @@ NB = N_ROWS // P
 TB = 4
 NT = NB // TB
 W = TB * P
-T1_FIRST = 0
-DLAG = 4
-T1_ON_VECTOR = [2, 6, 10, 14]
-BATCH_ENDS = [3, 7, 11, 13, 14, 15]
+PSUM_BANKS = 8
+
+TRAIL = 4
+SQ_LAG = 2
+X_COPY_ON_VECTOR = [2, 6, 10, 14]
+Q_BATCHES = [(0, 4), (4, 8), (8, 12), (12, 14), (14, 15), (15, 16)]
 
 FLOPS = 2 * N_ROWS * (D_IN * H0 + H0 * H1 + H1 * KC)
 
@@ -37,14 +39,12 @@ def tile_lintrans_pa_t_kernel(tc, x, W1, b1, W2, b2, clusters, out_0, out_1):
         xin_pool = es.enter_context(tc.tile_pool(name="xin", bufs=NT))
         work = es.enter_context(tc.tile_pool(name="work", bufs=3))
         work3 = es.enter_context(tc.tile_pool(name="work3", bufs=3))
-        zpool = es.enter_context(tc.tile_pool(name="zpool", bufs=DLAG + 4))
-        hqpool = es.enter_context(tc.tile_pool(name="hqpool", bufs=DLAG + 3))
-        psum = es.enter_context(tc.psum_pool(name="psum", bufs=8))
-        n_banks = [0]
+        zpool = es.enter_context(tc.tile_pool(name="zpool", bufs=TRAIL + SQ_LAG + 4))
+        upool = es.enter_context(tc.tile_pool(name="upool", bufs=SQ_LAG + 3))
+        hqpool = es.enter_context(tc.tile_pool(name="hqpool", bufs=TRAIL + 3))
+        psum = es.enter_context(tc.psum_pool(name="psum", bufs=PSUM_BANKS))
 
         def bank(shape):
-            k = n_banks[0] % 8
-            n_banks[0] += 1
             return psum.tile(shape, F32, tag="bank", name="bank")
 
         ident = keep.tile([P, P], F32)
@@ -52,31 +52,30 @@ def tile_lintrans_pa_t_kernel(tc, x, W1, b1, W2, b2, clusters, out_0, out_1):
 
         xin = []
 
-        def load_x(i):
-            t = xin_pool.tile([P, TB, D_IN], BF16, name="xin")
-            nc.sync.dma_start(out=t[:], in_=x_v[:, TB * i:TB * (i + 1), :])
-            xin.append(t)
+        def load_x(i, pieces):
+            rows = xin_pool.tile([P, TB, D_IN], BF16, name="xin")
+            step = TB // pieces
+            for b in range(0, TB, step):
+                nc.sync.dma_start(out=rows[:, b:b + step, :], in_=x_v[:, TB * i + b:TB * i + b + step, :])
+            xin.append(rows)
 
-        load_x(0)
+        load_x(0, 2)
         w1raw = keep.tile([P, 4, H0], BF16)
-        for u in range(2):
-            nc.sync.dma_start(
-                out=w1raw[:, 2 * u:2 * u + 2, :],
-                in_=W1[256 * u:256 * (u + 1), :].rearrange("(q e) c -> q e c", e=2),
-            )
+        nc.sync.dma_start(out=w1raw[:].rearrange("q (u e) c -> q u e c", u=2),
+                          in_=W1.rearrange("(u q e) c -> q u e c", u=2, e=2))
+        load_x(1, 1)
+        w2raw = keep.tile([P, 4, H1], BF16)
+        nc.sync.dma_start(out=w2raw[:], in_=W2.rearrange("(p m) j -> p m j", m=4))
         b1raw = keep.tile([P, 4], BF16)
         nc.scalar.dma_start(out=b1raw[:], in_=b1.rearrange("(p m) -> p m", m=4))
-        w2raw = keep.tile([P, 4, H1], BF16)
-        nc.scalar.dma_start(out=w2raw[:], in_=W2.rearrange("(p m) j -> p m j", m=4))
         par = keep.tile([P, P], BF16)
         nc.vector.memset(par[:], 0.0)
         nc.scalar.dma_start(out=par[0:KC, :], in_=clusters[:, 0:P])
         nc.scalar.dma_start(out=par[32:32 + KC, :], in_=clusters[:, P:2 * P])
-        nc.scalar.dma_start(out=par[64:66, :], in_=b2.rearrange("(h j) -> h j", j=P))
+        nc.scalar.dma_start(out=par[64:66, :], in_=b2.rearrange("(half j) -> half j", j=P))
         b2bc = keep.tile([P, H1], BF16)
-        nc.scalar.dma_start(out=b2bc[:], in_=b2.partition_broadcast(P))
-        for i in range(1, NT):
-            load_x(i)
+        for i in range(2, NT):
+            load_x(i, 1)
 
         ones = keep.tile([P, P], F32)
         nc.vector.memset(ones[:], 1.0)
@@ -96,7 +95,7 @@ def tile_lintrans_pa_t_kernel(tc, x, W1, b1, W2, b2, clusters, out_0, out_1):
         den = keep.tile([P, NB, KC], F32)
         rsum = keep.tile([P, NB], F32)
 
-        def setup_w1():
+        def quantise_w1():
             nc.vector.tensor_copy(
                 out=w1g[:].rearrange("q (m p) t -> q m p t", m=4),
                 in_=w1raw[:].rearrange("q t (p m) -> q m p t", m=4),
@@ -105,32 +104,37 @@ def tile_lintrans_pa_t_kernel(tc, x, W1, b1, W2, b2, clusters, out_0, out_1):
             nc.vector.quantize_mx(out=w1q[:].bitcast(FP8X4), scales=w1s[:],
                                   in_=w1g[:].rearrange("q c t -> q (c t)"))
 
-        def setup_w2():
+        def regroup_w2():
             nc.vector.tensor_copy(out=w2g[:], in_=w2raw[:].rearrange("p m j -> p j m"))
 
-        def setup_w2q():
+        def quantise_w2():
             nc.vector.quantize_mx(out=w2q[:].bitcast(FP8X4), scales=w2s[:],
                                   in_=w2g[:].rearrange("p j m -> p (j m)"))
 
-        def setup_consts():
+        def distance_constants():
             parf = keep.tile([P, P], F32)
             nc.vector.tensor_copy(out=parf[:], in_=par[:])
             par_ps = bank([P, P])
             nc.tensor.transpose(par_ps[:], parf[:], ident[:])
+            b2_ps = bank([P, 2, P])
+            for half in range(2):
+                nc.tensor.matmul(b2_ps[:, half, :], lhsT=ident[:, 64 + half:65 + half].to_broadcast([P, P]),
+                                 rhs=parf[:], start=True, stop=True)
+            nc.vector.tensor_copy(out=b2bc[:], in_=b2_ps[:].rearrange("p half j -> p (half j)"))
             cst = keep.tile([P, P], F32)
             nc.vector.tensor_copy(out=cst[:], in_=par_ps[:])
-            cT = cst[:, 0:64].rearrange("p (h k) -> p h k", h=2)[:, :, 0:KC]
+            cT = cst[:, 0:64].rearrange("p (half k) -> p half k", half=2)[:, :, 0:KC]
             nc.vector.tensor_scalar(out=m2cT[:], in0=cT, scalar1=-2.0, scalar2=None, op0=ALU.mult)
             b2x2 = keep.tile([P, 2], F32)
             nc.vector.tensor_scalar(out=b2x2[:], in0=cst[:, 64:66], scalar1=2.0, scalar2=None, op0=ALU.mult)
             cw = keep.tile([P, 2, KC], F32)
-            for h in range(2):
-                nc.vector.tensor_scalar(out=cw[:, h, :], in0=cT[:, h, :], scalar1=b2x2[:, h:h + 1],
+            for half in range(2):
+                nc.vector.tensor_scalar(out=cw[:, half, :], in0=cT[:, half, :], scalar1=b2x2[:, half:half + 1],
                                         scalar2=None, op0=ALU.subtract)
             nc.vector.tensor_tensor(out=cw[:], in0=cw[:], in1=cT, op=ALU.mult)
             e_ps = bank([P, KC])
-            for h in range(2):
-                nc.tensor.matmul(e_ps[:], lhsT=ones[:], rhs=cw[:, h, :], start=(h == 0), stop=(h == 1))
+            for half in range(2):
+                nc.tensor.matmul(e_ps[:], lhsT=ones[:], rhs=cw[:, half, :], start=(half == 0), stop=(half == 1))
             nc.vector.tensor_scalar(out=e_bc[:], in0=e_ps[:], scalar1=1.0, scalar2=None, op0=ALU.add)
             term = keep.tile([P, 3, KC], BF16)
             for g in range(3):
@@ -148,7 +152,7 @@ def tile_lintrans_pa_t_kernel(tc, x, W1, b1, W2, b2, clusters, out_0, out_1):
         def ok(i):
             return 0 <= i < NT
 
-        def fA(i):
+        def transpose_x(i):
             xf = xin[i][:].bitcast(F32)
             for pr in range(2):
                 xt = bank([P, 2, 2, P])
@@ -157,25 +161,25 @@ def tile_lintrans_pa_t_kernel(tc, x, W1, b1, W2, b2, clusters, out_0, out_1):
                     for u in range(2):
                         nc.tensor.transpose(xt[:, bb, u, :], xf[:, 2 * pr + bb, P * u:P * (u + 1)], ident[:])
 
-        def fT1(i, pr):
-            if pr == T1_FIRST:
+        def copy_x(i, pr):
+            if pr == 0:
                 xg = work.tile([P, W * 4], BF16, align_bytes=64, name="xg")
                 st[("xg", i)] = xg
             xg = st[("xg", i)]
             xgf = xg[:].bitcast(F32).rearrange("p (b n u) -> p b n u", b=TB, u=2)
             src = st[("xt", i, pr)][:].rearrange("p b u n -> p b n u")
-            if pr == 0 and i in T1_ON_VECTOR:
+            if pr == 0 and i in X_COPY_ON_VECTOR:
                 nc.vector.tensor_copy(out=xgf[:, 2 * pr:2 * pr + 2, :, :], in_=src)
             else:
                 nc.scalar.copy(out=xgf[:, 2 * pr:2 * pr + 2, :, :], in_=src)
 
-        def fT2(i):
+        def quantise_x(i):
             xq = work3.tile([P, W], U32, align_bytes=64, name="xq")
             xs = work3.tile([P, W], U8, align_bytes=64, name="xs")
             st[("xq", i)] = (xq, xs)
             nc.vector.quantize_mx(out=xq[:].bitcast(FP8X4), scales=xs[:], in_=st[("xg", i)][:])
 
-        def fB(i, m):
+        def layer1(i, m):
             xq, xs = st[("xq", i)]
             hp = bank([P, W])
             st[("hp", i, m)] = hp
@@ -183,26 +187,26 @@ def tile_lintrans_pa_t_kernel(tc, x, W1, b1, W2, b2, clusters, out_0, out_1):
                                 lhsT_scale=w1s[:, P * m:P * (m + 1)],
                                 rhs=xq[:].bitcast(FP8X4), rhs_scale=xs[:], start=True, stop=True)
 
-        def fT3(i, m):
+        def silu(i, m):
             if m == 0:
                 st[("hb", i)] = work.tile([P, 4, W], BF16, name="hb")
             nc.scalar.activation(out=st[("hb", i)][:, m, :], in_=st[("hp", i, m)][:], func=ACT.Silu,
                                  bias=b1col[:, m:m + 1], scale=1.0)
 
-        def fT4(i):
+        def regroup_h(i):
             hg = work.tile([P, W, 4], BF16, align_bytes=64, name="hg")
             st[("hg", i)] = hg
             nc.vector.tensor_copy(out=hg[:].rearrange("p (c i) t -> p c t i", i=4),
                                   in_=st[("hb", i)][:].rearrange("p t (c i) -> p c t i", i=4))
 
-        def fT5(i):
+        def quantise_h(i):
             hq = hqpool.tile([P, W], U32, align_bytes=64, name="hq")
             hs = hqpool.tile([P, W], U8, align_bytes=64, name="hs")
             st[("hq", i)] = (hq, hs)
             nc.vector.quantize_mx(out=hq[:].bitcast(FP8X4), scales=hs[:],
                                   in_=st[("hg", i)][:].rearrange("p n t -> p (n t)"))
 
-        def fC(i, pr):
+        def layer2_rows(i, pr):
             hq, hs = st[("hq", i)]
             up = bank([P, 2, H1])
             st[("up", i, pr)] = up
@@ -212,15 +216,15 @@ def tile_lintrans_pa_t_kernel(tc, x, W1, b1, W2, b2, clusters, out_0, out_1):
                                     lhsT_scale=hs[:, P * blk:P * (blk + 1)],
                                     rhs=w2q[:].bitcast(FP8X4), rhs_scale=w2s[:], start=True, stop=True)
 
-        def fD(i, h):
+        def layer2_transposed(i, half):
             hq, hs = st[("hq", i)]
             ut = bank([P, W])
-            st[("ut", i, h)] = ut
-            nc.tensor.matmul_mx(out=ut[:], lhsT=w2q[:, P * h:P * (h + 1)].bitcast(FP8X4),
-                                lhsT_scale=w2s[:, P * h:P * (h + 1)],
+            st[("ut", i, half)] = ut
+            nc.tensor.matmul_mx(out=ut[:], lhsT=w2q[:, P * half:P * (half + 1)].bitcast(FP8X4),
+                                lhsT_scale=w2s[:, P * half:P * (half + 1)],
                                 rhs=hq[:].bitcast(FP8X4), rhs_scale=hs[:], start=True, stop=True)
 
-        def fT6(i, pr):
+        def add_b2_and_store(i, pr):
             if pr == 0:
                 st[("z", i)] = zpool.tile([P, TB, H1], F32, name="zsb")
             nc.vector.tensor_tensor(out=st[("z", i)][:, 2 * pr:2 * pr + 2, :], in0=st[("up", i, pr)][:],
@@ -228,43 +232,42 @@ def tile_lintrans_pa_t_kernel(tc, x, W1, b1, W2, b2, clusters, out_0, out_1):
             if pr == 1:
                 nc.sync.dma_start(out=z_v[:, TB * i:TB * (i + 1), :], in_=st[("z", i)][:])
 
-        def fT7(i, h):
-            if h == 0:
-                st[("uh", i)] = work.tile([P, 2, W], BF16, name="uh")
-            nc.scalar.copy(out=st[("uh", i)][:, h, :], in_=st[("ut", i, h)][:])
+        def take_hi(i, half):
+            if half == 0:
+                st[("uh", i)] = upool.tile([P, 2, W], BF16, name="uh")
+            nc.scalar.copy(out=st[("uh", i)][:, half, :], in_=st[("ut", i, half)][:])
 
-        def fT7lo(i, h):
-            if h == 0:
-                st[("ul", i)] = work.tile([P, 2, W], BF16, name="ul")
-            nc.vector.tensor_tensor(out=st[("ul", i)][:, h, :], in0=st[("ut", i, h)][:],
-                                    in1=st[("uh", i)][:, h, :], op=ALU.subtract)
+        def take_lo(i, half):
+            if half == 0:
+                st[("ul", i)] = upool.tile([P, 2, W], BF16, name="ul")
+            nc.vector.tensor_tensor(out=st[("ul", i)][:, half, :], in0=st[("ut", i, half)][:],
+                                    in1=st[("uh", i)][:, half, :], op=ALU.subtract)
 
-        def fT8(i):
+        def sum_squares(i):
             for blk in range(TB):
                 junk = work.tile([P, H1], BF16, name="junk")
                 nc.scalar.activation(out=junk[:], in_=st[("z", i)][:, blk, :], func=ACT.Square,
                                      accum_out=ssq[:, TB * i + blk:TB * i + blk + 1])
 
-        def fE(i):
+        def distances(i):
             dp = bank([P, TB, KC])
             st[("dp", i)] = dp
-            parts = (st[("uh", i)], st[("ul", i)])
             for blk in range(TB):
-                for n in range(4):
-                    h = n // 2
-                    nc.tensor.matmul(dp[:, blk, :], lhsT=parts[n % 2][:, h, P * blk:P * (blk + 1)],
-                                     rhs=m2cT[:, h, :], start=(n == 0), stop=False)
+                for half in range(2):
+                    for which, term_of_u in enumerate((st[("uh", i)], st[("ul", i)])):
+                        nc.tensor.matmul(dp[:, blk, :], lhsT=term_of_u[:, half, P * blk:P * (blk + 1)],
+                                         rhs=m2cT[:, half, :], start=(half == 0 and which == 0), stop=False)
                 nc.tensor.matmul(dp[:, blk, :], lhsT=pick[:].to_broadcast([P, P]), rhs=e_rows[:],
                                  start=False, stop=True)
 
-        def fT9(i):
+        def student_t(i):
             d = den[:, TB * i:TB * (i + 1), :]
             nc.vector.tensor_tensor(out=d, in0=st[("dp", i)][:],
                                     in1=ssq[:, TB * i:TB * (i + 1)].unsqueeze(2).to_broadcast([P, TB, KC]),
                                     op=ALU.add)
             nc.vector.reciprocal(out=d, in_=d)
 
-        def finish(b0, b9):
+        def normalise_and_store(b0, b9):
             nb = b9 - b0
             d = den[:, b0:b9, :]
             nc.vector.tensor_reduce(out=rsum[:, b0:b9], in_=d, axis=AX.X, op=ALU.add)
@@ -273,51 +276,54 @@ def tile_lintrans_pa_t_kernel(tc, x, W1, b1, W2, b2, clusters, out_0, out_1):
                                     op=ALU.mult)
             nc.sync.dma_start(out=q_v[:, b0:b9, :], in_=d)
 
-        setup_w1()
-        first = [0]
-        for p in range(NT + 6 + DLAG):
-            d = p - 4 - DLAG
-            if ok(p - 3):
-                fT4(p - 3)
-            if ok(p - 2):
+        batch_start = {}
+        for t0, t9 in Q_BATCHES:
+            batch_start[t9 - 1] = t0
+
+        quantise_w1()
+        for s in range(NT + 5 + TRAIL + SQ_LAG):
+            far = s - 4 - TRAIL
+            sq = far - SQ_LAG
+            if ok(s - 3):
+                regroup_h(s - 3)
+            if ok(s - 2):
                 for m in range(4):
-                    fB(p - 2, m)
+                    layer1(s - 2, m)
                 for m in range(4):
-                    fT3(p - 2, m)
-            if ok(p - 1):
-                fT2(p - 1)
-            if p == 1:
-                setup_w2()
-            if ok(p - 4):
-                fC(p - 4, 0)
-                fC(p - 4, 1)
-            if ok(d):
-                fD(d, 0)
-                fD(d, 1)
-            if ok(p - 3):
-                fT5(p - 3)
-            if ok(p - 4):
-                fT6(p - 4, 0)
-                fT6(p - 4, 1)
-            if ok(d - 1):
-                fE(d - 1)
-            if ok(d):
-                fT7(d, 0)
-                fT7(d, 1)
-                fT7lo(d, 0)
-                fT7lo(d, 1)
-            if p == 2:
-                setup_w2q()
-                setup_consts()
-            if ok(p):
-                fA(p)
-            if ok(d - 1):
-                fT9(d - 1)
-                if (d - 1) in BATCH_ENDS:
-                    finish(TB * first[0], TB * d)
-                    first[0] = d
-            if ok(d):
-                fT8(d)
-            if ok(p):
-                fT1(p, 0)
-                fT1(p, 1)
+                    silu(s - 2, m)
+            if ok(s - 1):
+                quantise_x(s - 1)
+            if s == 1:
+                regroup_w2()
+            if ok(s - 4):
+                layer2_rows(s - 4, 0)
+                layer2_rows(s - 4, 1)
+            if ok(far):
+                layer2_transposed(far, 0)
+                layer2_transposed(far, 1)
+            if ok(s - 3):
+                quantise_h(s - 3)
+            if ok(s - 4):
+                add_b2_and_store(s - 4, 0)
+                add_b2_and_store(s - 4, 1)
+            if ok(sq):
+                distances(sq)
+            if ok(far):
+                take_hi(far, 0)
+                take_hi(far, 1)
+                take_lo(far, 0)
+                take_lo(far, 1)
+            if s == 2:
+                quantise_w2()
+                distance_constants()
+            if ok(s):
+                transpose_x(s)
+            if ok(sq - 1):
+                student_t(sq - 1)
+                if (sq - 1) in batch_start:
+                    normalise_and_store(TB * batch_start[sq - 1], TB * sq)
+            if ok(sq):
+                sum_squares(sq)
+            if ok(s):
+                copy_x(s, 0)
+                copy_x(s, 1)

@@ -52,30 +52,31 @@ def tile_lintrans_pa_t_kernel(tc, x, W1, b1, W2, b2, clusters, out_0, out_1):
 
         xin = []
 
-        def load_x(i, pieces):
+        def load_x(i):
             rows = xin_pool.tile([P, TB, D_IN], BF16, name="xin")
-            step = TB // pieces
-            for b in range(0, TB, step):
-                nc.sync.dma_start(out=rows[:, b:b + step, :], in_=x_v[:, TB * i + b:TB * i + b + step, :])
+            nc.sync.dma_start(out=rows[:], in_=x_v[:, TB * i:TB * (i + 1), :])
             xin.append(rows)
 
-        load_x(0, 2)
+        load_x(0)
         w1raw = keep.tile([P, 4, H0], BF16)
-        nc.sync.dma_start(out=w1raw[:].rearrange("q (u e) c -> q u e c", u=2),
-                          in_=W1.rearrange("(u q e) c -> q u e c", u=2, e=2))
-        load_x(1, 1)
-        w2raw = keep.tile([P, 4, H1], BF16)
-        nc.sync.dma_start(out=w2raw[:], in_=W2.rearrange("(p m) j -> p m j", m=4))
+        for u in range(2):
+            nc.sync.dma_start(
+                out=w1raw[:, 2 * u:2 * u + 2, :],
+                in_=W1[256 * u:256 * (u + 1), :].rearrange("(q e) c -> q e c", e=2),
+            )
         b1raw = keep.tile([P, 4], BF16)
         nc.scalar.dma_start(out=b1raw[:], in_=b1.rearrange("(p m) -> p m", m=4))
+        w2raw = keep.tile([P, 4, H1], BF16)
+        nc.scalar.dma_start(out=w2raw[:], in_=W2.rearrange("(p m) j -> p m j", m=4))
         par = keep.tile([P, P], BF16)
         nc.vector.memset(par[:], 0.0)
         nc.scalar.dma_start(out=par[0:KC, :], in_=clusters[:, 0:P])
         nc.scalar.dma_start(out=par[32:32 + KC, :], in_=clusters[:, P:2 * P])
         nc.scalar.dma_start(out=par[64:66, :], in_=b2.rearrange("(half j) -> half j", j=P))
         b2bc = keep.tile([P, H1], BF16)
-        for i in range(2, NT):
-            load_x(i, 1)
+        nc.scalar.dma_start(out=b2bc[:], in_=b2.partition_broadcast(P))
+        for i in range(1, NT):
+            load_x(i)
 
         ones = keep.tile([P, P], F32)
         nc.vector.memset(ones[:], 1.0)
@@ -116,11 +117,6 @@ def tile_lintrans_pa_t_kernel(tc, x, W1, b1, W2, b2, clusters, out_0, out_1):
             nc.vector.tensor_copy(out=parf[:], in_=par[:])
             par_ps = bank([P, P])
             nc.tensor.transpose(par_ps[:], parf[:], ident[:])
-            b2_ps = bank([P, 2, P])
-            for half in range(2):
-                nc.tensor.matmul(b2_ps[:, half, :], lhsT=ident[:, 64 + half:65 + half].to_broadcast([P, P]),
-                                 rhs=parf[:], start=True, stop=True)
-            nc.vector.tensor_copy(out=b2bc[:], in_=b2_ps[:].rearrange("p half j -> p (half j)"))
             cst = keep.tile([P, P], F32)
             nc.vector.tensor_copy(out=cst[:], in_=par_ps[:])
             cT = cst[:, 0:64].rearrange("p (half k) -> p half k", half=2)[:, :, 0:KC]

@@ -22,7 +22,7 @@ PSUM_BANKS = 8
 
 TRAIL = 4
 SQ_LAG = 2
-X_COPY_ON_VECTOR = [2, 6, 10, 14]
+X_COPY_ON_VECTOR = [6, 10, 14]
 Q_BATCHES = [(0, 4), (4, 8), (8, 12), (12, 14), (14, 15), (15, 16)]
 
 FLOPS = 2 * N_ROWS * (D_IN * H0 + H0 * H1 + H1 * KC)
@@ -68,6 +68,9 @@ def tile_lintrans_pa_t_kernel(tc, x, W1, b1, W2, b2, clusters, out_0, out_1):
         nc.scalar.dma_start(out=b1raw[:], in_=b1.rearrange("(p m) -> p m", m=4))
         w2raw = keep.tile([P, 4, H1], BF16)
         nc.scalar.dma_start(out=w2raw[:], in_=W2.rearrange("(p m) j -> p m j", m=4))
+        warm = keep.tile([P, 1], F32)
+        nc.vector.memset(warm[:], 0.0)
+        nc.scalar.activation(out=warm[:], in_=warm[:], func=ACT.Silu)
         par = keep.tile([P, P], BF16)
         nc.vector.memset(par[:], 0.0)
         nc.scalar.dma_start(out=par[0:KC, :], in_=clusters[:, 0:P])
@@ -96,14 +99,15 @@ def tile_lintrans_pa_t_kernel(tc, x, W1, b1, W2, b2, clusters, out_0, out_1):
         den = keep.tile([P, NB, KC], F32)
         rsum = keep.tile([P, NB], F32)
 
-        def quantise_w1():
-            nc.vector.tensor_copy(
-                out=w1g[:].rearrange("q (m p) t -> q m p t", m=4),
-                in_=w1raw[:].rearrange("q t (p m) -> q m p t", m=4),
-            )
-            nc.vector.tensor_copy(out=b1col[:], in_=b1raw[:])
-            nc.vector.quantize_mx(out=w1q[:].bitcast(FP8X4), scales=w1s[:],
-                                  in_=w1g[:].rearrange("q c t -> q (c t)"))
+        def regroup_w1(m):
+            nc.vector.tensor_copy(out=w1g[:, P * m:P * (m + 1), :],
+                                  in_=w1raw[:].rearrange("q t (p m) -> q m p t", m=4)[:, m])
+
+        def quantise_w1(m):
+            nc.vector.quantize_mx(out=w1q[:, P * m:P * (m + 1)].bitcast(FP8X4), scales=w1s[:, P * m:P * (m + 1)],
+                                  in_=w1g[:, P * m:P * (m + 1), :].rearrange("q c t -> q (c t)"))
+
+        st = {}
 
         def regroup_w2():
             nc.vector.tensor_copy(out=w2g[:], in_=w2raw[:].rearrange("p m j -> p j m"))
@@ -112,26 +116,35 @@ def tile_lintrans_pa_t_kernel(tc, x, W1, b1, W2, b2, clusters, out_0, out_1):
             nc.vector.quantize_mx(out=w2q[:].bitcast(FP8X4), scales=w2s[:],
                                   in_=w2g[:].rearrange("p j m -> p (j m)"))
 
-        def distance_constants():
-            parf = keep.tile([P, P], F32)
+        parf = keep.tile([P, P], F32)
+        cst = keep.tile([P, P], F32)
+        cw = keep.tile([P, 2, KC], F32)
+
+        def constants_to_f32():
             nc.vector.tensor_copy(out=parf[:], in_=par[:])
-            par_ps = bank([P, P])
-            nc.tensor.transpose(par_ps[:], parf[:], ident[:])
-            cst = keep.tile([P, P], F32)
-            nc.vector.tensor_copy(out=cst[:], in_=par_ps[:])
+
+        def constants_transpose():
+            st["par_ps"] = bank([P, P])
+            nc.tensor.transpose(st["par_ps"][:], parf[:], ident[:])
+
+        def constants_products():
+            nc.vector.tensor_copy(out=cst[:], in_=st["par_ps"][:])
             cT = cst[:, 0:64].rearrange("p (half k) -> p half k", half=2)[:, :, 0:KC]
             nc.vector.tensor_scalar(out=m2cT[:], in0=cT, scalar1=-2.0, scalar2=None, op0=ALU.mult)
             b2x2 = keep.tile([P, 2], F32)
             nc.vector.tensor_scalar(out=b2x2[:], in0=cst[:, 64:66], scalar1=2.0, scalar2=None, op0=ALU.mult)
-            cw = keep.tile([P, 2, KC], F32)
             for half in range(2):
                 nc.vector.tensor_scalar(out=cw[:, half, :], in0=cT[:, half, :], scalar1=b2x2[:, half:half + 1],
                                         scalar2=None, op0=ALU.subtract)
             nc.vector.tensor_tensor(out=cw[:], in0=cw[:], in1=cT, op=ALU.mult)
-            e_ps = bank([P, KC])
+
+        def constants_sum():
+            st["e_ps"] = bank([P, KC])
             for half in range(2):
-                nc.tensor.matmul(e_ps[:], lhsT=ones[:], rhs=cw[:, half, :], start=(half == 0), stop=(half == 1))
-            nc.vector.tensor_scalar(out=e_bc[:], in0=e_ps[:], scalar1=1.0, scalar2=None, op0=ALU.add)
+                nc.tensor.matmul(st["e_ps"][:], lhsT=ones[:], rhs=cw[:, half, :], start=(half == 0), stop=(half == 1))
+
+        def constants_terms():
+            nc.vector.tensor_scalar(out=e_bc[:], in0=st["e_ps"][:], scalar1=1.0, scalar2=None, op0=ALU.add)
             term = keep.tile([P, 3, KC], BF16)
             for g in range(3):
                 nc.vector.tensor_copy(out=term[:, g, :], in_=e_bc[:])
@@ -142,8 +155,6 @@ def tile_lintrans_pa_t_kernel(tc, x, W1, b1, W2, b2, clusters, out_0, out_1):
                 nc.vector.tensor_copy(out=e_rows[rows, :], in_=term[rows, g, :])
             nc.vector.tensor_tensor(out=pick[:], in0=ident[:, 0:1], in1=ident[:, 32:33], op=ALU.add)
             nc.vector.tensor_tensor(out=pick[:], in0=pick[:], in1=ident[:, 64:65], op=ALU.add)
-
-        st = {}
 
         def ok(i):
             return 0 <= i < NT
@@ -276,10 +287,17 @@ def tile_lintrans_pa_t_kernel(tc, x, W1, b1, W2, b2, clusters, out_0, out_1):
         for t0, t9 in Q_BATCHES:
             batch_start[t9 - 1] = t0
 
-        quantise_w1()
+        regroup_w1(0)
+        nc.vector.tensor_copy(out=b1col[:], in_=b1raw[:])
+        quantise_w1(0)
+        regroup_w1(1)
         for s in range(NT + 5 + TRAIL + SQ_LAG):
             far = s - 4 - TRAIL
             sq = far - SQ_LAG
+            if s == 4:
+                constants_products()
+            if s == 6:
+                constants_terms()
             if ok(s - 3):
                 regroup_h(s - 3)
             if ok(s - 2):
@@ -290,6 +308,11 @@ def tile_lintrans_pa_t_kernel(tc, x, W1, b1, W2, b2, clusters, out_0, out_1):
             if ok(s - 1):
                 quantise_x(s - 1)
             if s == 1:
+                quantise_w1(1)
+                regroup_w1(2)
+                regroup_w1(3)
+                quantise_w1(2)
+                quantise_w1(3)
                 regroup_w2()
             if ok(s - 4):
                 layer2_rows(s - 4, 0)
@@ -311,7 +334,11 @@ def tile_lintrans_pa_t_kernel(tc, x, W1, b1, W2, b2, clusters, out_0, out_1):
                 take_lo(far, 1)
             if s == 2:
                 quantise_w2()
-                distance_constants()
+                constants_to_f32()
+            if s == 3:
+                constants_transpose()
+            if s == 5:
+                constants_sum()
             if ok(s):
                 transpose_x(s)
             if ok(sq - 1):

@@ -16,14 +16,22 @@ P = 128
 N_ROWS, D_IN, H0, H1, KC = 8192, 512, 512, 256, 20
 NB = N_ROWS // P
 TB = 4
-NT = NB // TB
 W = TB * P
+SIZES = [2, 2] + [TB] * 14 + [2, 2]
+NT = len(SIZES)
+FIRST = [sum(SIZES[:i]) for i in range(NT + 1)]
 PSUM_BANKS = 8
 
 TRAIL = 4
 SQ_LAG = 2
-X_COPY_ON_VECTOR = [6, 10, 14]
-Q_BATCHES = [(0, 4), (4, 8), (8, 12), (12, 14), (14, 15), (15, 16)]
+X_COPY_ON_VECTOR = []
+F32_GROUPS = [(2, 6), (6, 10)]
+U_ON_SCALAR = [3, 5, 7]
+SLOT = 32
+Q_BATCHES = [(0, 6), (6, 10), (10, 13), (13, 15), (15, 16), (16, 17), (17, 18)]
+
+WARM_UP = 6
+HEAD = 3
 
 FLOPS = 2 * N_ROWS * (D_IN * H0 + H0 * H1 + H1 * KC)
 
@@ -42,10 +50,14 @@ def tile_lintrans_pa_t_kernel(tc, x, W1, b1, W2, b2, clusters, out_0, out_1):
         zpool = es.enter_context(tc.tile_pool(name="zpool", bufs=TRAIL + SQ_LAG + 4))
         upool = es.enter_context(tc.tile_pool(name="upool", bufs=SQ_LAG + 3))
         hqpool = es.enter_context(tc.tile_pool(name="hqpool", bufs=TRAIL + 3))
+        sepool = es.enter_context(tc.tile_pool(name="sepool", bufs=6))
         psum = es.enter_context(tc.psum_pool(name="psum", bufs=PSUM_BANKS))
 
         def bank(shape):
             return psum.tile(shape, F32, tag="bank", name="bank")
+
+        zeros = keep.tile([P, 2 * P], BF16)
+        nc.vector.memset(zeros[:], 0.0)
 
         ident = keep.tile([P, P], F32)
         make_identity(nc, ident[:])
@@ -53,8 +65,8 @@ def tile_lintrans_pa_t_kernel(tc, x, W1, b1, W2, b2, clusters, out_0, out_1):
         xin = []
 
         def load_x(i):
-            rows = xin_pool.tile([P, TB, D_IN], BF16, name="xin")
-            nc.sync.dma_start(out=rows[:], in_=x_v[:, TB * i:TB * (i + 1), :])
+            rows = xin_pool.tile([P, SIZES[i], D_IN], BF16, name="xin")
+            nc.sync.dma_start(out=rows[:], in_=x_v[:, FIRST[i]:FIRST[i + 1], :])
             xin.append(rows)
 
         load_x(0)
@@ -66,23 +78,27 @@ def tile_lintrans_pa_t_kernel(tc, x, W1, b1, W2, b2, clusters, out_0, out_1):
             )
         b1raw = keep.tile([P, 4], BF16)
         nc.scalar.dma_start(out=b1raw[:], in_=b1.rearrange("(p m) -> p m", m=4))
-        w2raw = keep.tile([P, 4, H1], BF16)
-        nc.scalar.dma_start(out=w2raw[:], in_=W2.rearrange("(p m) j -> p m j", m=4))
         warm = keep.tile([P, 1], F32)
         nc.vector.memset(warm[:], 0.0)
         nc.scalar.activation(out=warm[:], in_=warm[:], func=ACT.Silu)
         par = keep.tile([P, P], BF16)
-        nc.vector.memset(par[:], 0.0)
-        nc.scalar.dma_start(out=par[0:KC, :], in_=clusters[:, 0:P])
-        nc.scalar.dma_start(out=par[32:32 + KC, :], in_=clusters[:, P:2 * P])
-        nc.scalar.dma_start(out=par[64:66, :], in_=b2.rearrange("(half j) -> half j", j=P))
+        nc.gpsimd.memset(par[:], 0.0)
+        nc.gpsimd.dma_start(out=par[0:KC, :], in_=clusters[:, 0:P])
+        nc.gpsimd.dma_start(out=par[32:32 + KC, :], in_=clusters[:, P:2 * P])
+        nc.gpsimd.dma_start(out=par[64:66, :], in_=b2.rearrange("(half j) -> half j", j=P))
+        load_x(1)
+        load_x(2)
+        w2raw = keep.tile([P, 4, H1], BF16)
+        nc.sync.dma_start(out=w2raw[:], in_=W2.rearrange("(p m) j -> p m j", m=4))
         b2bc = keep.tile([P, H1], BF16)
-        nc.scalar.dma_start(out=b2bc[:], in_=b2.partition_broadcast(P))
-        for i in range(1, NT):
+        nc.sync.dma_start(out=b2bc[:], in_=b2.partition_broadcast(P))
+        for i in range(3, NT):
             load_x(i)
 
         ones = keep.tile([P, P], F32)
-        nc.vector.memset(ones[:], 1.0)
+        nc.gpsimd.memset(ones[:], 1.0)
+        wide = keep.tile([P, 2, P + 3 * SLOT], F32)
+        nc.gpsimd.memset(wide[:], 0.0)
 
         w1g = keep.tile([P, H0, 4], BF16, align_bytes=64)
         w1q = keep.tile([P, H0], U32, align_bytes=64)
@@ -93,15 +109,17 @@ def tile_lintrans_pa_t_kernel(tc, x, W1, b1, W2, b2, clusters, out_0, out_1):
         w2s = keep.tile([P, H1], U8, align_bytes=64)
         m2cT = keep.tile([P, 2, KC], BF16)
         e_bc = keep.tile([P, KC], F32)
-        e_rows = keep.tile([P, KC], BF16)
-        pick = keep.tile([P, 1], BF16)
         ssq = keep.tile([P, NB], F32)
         den = keep.tile([P, NB, KC], F32)
         rsum = keep.tile([P, NB], F32)
 
         def regroup_w1(m):
-            nc.vector.tensor_copy(out=w1g[:, P * m:P * (m + 1), :],
-                                  in_=w1raw[:].rearrange("q t (p m) -> q m p t", m=4)[:, m])
+            part = w1g[:, P * m:P * (m + 1), :]
+            raw = w1raw[:].rearrange("q t (p m) -> q m p t", m=4)[:, m]
+            if m % 2:
+                nc.scalar.copy(out=part, in_=raw)
+            else:
+                nc.vector.tensor_copy(out=part, in_=raw)
 
         def quantise_w1(m):
             nc.vector.quantize_mx(out=w1q[:, P * m:P * (m + 1)].bitcast(FP8X4), scales=w1s[:, P * m:P * (m + 1)],
@@ -121,7 +139,7 @@ def tile_lintrans_pa_t_kernel(tc, x, W1, b1, W2, b2, clusters, out_0, out_1):
         cw = keep.tile([P, 2, KC], F32)
 
         def constants_to_f32():
-            nc.vector.tensor_copy(out=parf[:], in_=par[:])
+            nc.gpsimd.tensor_copy(out=parf[:], in_=par[:])
 
         def constants_transpose():
             st["par_ps"] = bank([P, P])
@@ -131,6 +149,8 @@ def tile_lintrans_pa_t_kernel(tc, x, W1, b1, W2, b2, clusters, out_0, out_1):
             nc.vector.tensor_copy(out=cst[:], in_=st["par_ps"][:])
             cT = cst[:, 0:64].rearrange("p (half k) -> p half k", half=2)[:, :, 0:KC]
             nc.vector.tensor_scalar(out=m2cT[:], in0=cT, scalar1=-2.0, scalar2=None, op0=ALU.mult)
+            nc.vector.tensor_scalar(out=wide[:, :, 3 * SLOT:3 * SLOT + KC], in0=cT, scalar1=-2.0, scalar2=None,
+                                    op0=ALU.mult)
             b2x2 = keep.tile([P, 2], F32)
             nc.vector.tensor_scalar(out=b2x2[:], in0=cst[:, 64:66], scalar1=2.0, scalar2=None, op0=ALU.mult)
             for half in range(2):
@@ -145,23 +165,31 @@ def tile_lintrans_pa_t_kernel(tc, x, W1, b1, W2, b2, clusters, out_0, out_1):
 
         def constants_terms():
             nc.vector.tensor_scalar(out=e_bc[:], in0=st["e_ps"][:], scalar1=1.0, scalar2=None, op0=ALU.add)
-            term = keep.tile([P, 3, KC], BF16)
-            for g in range(3):
-                nc.vector.tensor_copy(out=term[:, g, :], in_=e_bc[:])
-                nc.vector.tensor_tensor(out=e_bc[:], in0=e_bc[:], in1=term[:, g, :], op=ALU.subtract)
-            nc.vector.memset(e_rows[:], 0.0)
-            for g in range(3):
-                rows = slice(32 * g, 32 * (g + 1))
-                nc.vector.tensor_copy(out=e_rows[rows, :], in_=term[rows, g, :])
-            nc.vector.tensor_tensor(out=pick[:], in0=ident[:, 0:1], in1=ident[:, 32:33], op=ALU.add)
-            nc.vector.tensor_tensor(out=pick[:], in0=pick[:], in1=ident[:, 64:65], op=ALU.add)
+
+        group_of = {}
+        for t0, t9 in F32_GROUPS:
+            for i in range(t0, t9):
+                group_of[i] = (t0, t9)
 
         def ok(i):
             return 0 <= i < NT
 
+        def rows_of(i):
+            return P * SIZES[i]
+
+        def pairs_of(i):
+            return range(SIZES[i] // 2)
+
+        def side_by_side(i, r):
+            n = rows_of(i)
+            per = W // n
+            if r % per == 0:
+                st["open"] = bank([P, W])
+            return st["open"][:, n * (r % per):n * (r % per + 1)]
+
         def transpose_x(i):
             xf = xin[i][:].bitcast(F32)
-            for pr in range(2):
+            for pr in pairs_of(i):
                 xt = bank([P, 2, 2, P])
                 st[("xt", i, pr)] = xt
                 for bb in range(2):
@@ -170,10 +198,10 @@ def tile_lintrans_pa_t_kernel(tc, x, W1, b1, W2, b2, clusters, out_0, out_1):
 
         def copy_x(i, pr):
             if pr == 0:
-                xg = work.tile([P, W * 4], BF16, align_bytes=64, name="xg")
+                xg = work.tile([P, rows_of(i) * 4], BF16, align_bytes=64, name="xg")
                 st[("xg", i)] = xg
             xg = st[("xg", i)]
-            xgf = xg[:].bitcast(F32).rearrange("p (b n u) -> p b n u", b=TB, u=2)
+            xgf = xg[:].bitcast(F32).rearrange("p (b n u) -> p b n u", b=SIZES[i], u=2)
             src = st[("xt", i, pr)][:].rearrange("p b u n -> p b n u")
             if pr == 0 and i in X_COPY_ON_VECTOR:
                 nc.vector.tensor_copy(out=xgf[:, 2 * pr:2 * pr + 2, :, :], in_=src)
@@ -181,34 +209,34 @@ def tile_lintrans_pa_t_kernel(tc, x, W1, b1, W2, b2, clusters, out_0, out_1):
                 nc.scalar.copy(out=xgf[:, 2 * pr:2 * pr + 2, :, :], in_=src)
 
         def quantise_x(i):
-            xq = work3.tile([P, W], U32, align_bytes=64, name="xq")
-            xs = work3.tile([P, W], U8, align_bytes=64, name="xs")
+            xq = work3.tile([P, rows_of(i)], U32, align_bytes=64, name="xq")
+            xs = work3.tile([P, rows_of(i)], U8, align_bytes=64, name="xs")
             st[("xq", i)] = (xq, xs)
             nc.vector.quantize_mx(out=xq[:].bitcast(FP8X4), scales=xs[:], in_=st[("xg", i)][:])
 
         def layer1(i, m):
             xq, xs = st[("xq", i)]
-            hp = bank([P, W])
+            hp = side_by_side(i, m)
             st[("hp", i, m)] = hp
-            nc.tensor.matmul_mx(out=hp[:], lhsT=w1q[:, P * m:P * (m + 1)].bitcast(FP8X4),
+            nc.tensor.matmul_mx(out=hp, lhsT=w1q[:, P * m:P * (m + 1)].bitcast(FP8X4),
                                 lhsT_scale=w1s[:, P * m:P * (m + 1)],
                                 rhs=xq[:].bitcast(FP8X4), rhs_scale=xs[:], start=True, stop=True)
 
         def silu(i, m):
             if m == 0:
-                st[("hb", i)] = work.tile([P, 4, W], BF16, name="hb")
-            nc.scalar.activation(out=st[("hb", i)][:, m, :], in_=st[("hp", i, m)][:], func=ACT.Silu,
+                st[("hb", i)] = work.tile([P, 4, rows_of(i)], BF16, name="hb")
+            nc.scalar.activation(out=st[("hb", i)][:, m, :], in_=st[("hp", i, m)], func=ACT.Silu,
                                  bias=b1col[:, m:m + 1], scale=1.0)
 
         def regroup_h(i):
-            hg = work.tile([P, W, 4], BF16, align_bytes=64, name="hg")
+            hg = work.tile([P, rows_of(i), 4], BF16, align_bytes=64, name="hg")
             st[("hg", i)] = hg
             nc.vector.tensor_copy(out=hg[:].rearrange("p (c i) t -> p c t i", i=4),
                                   in_=st[("hb", i)][:].rearrange("p t (c i) -> p c t i", i=4))
 
         def quantise_h(i):
-            hq = hqpool.tile([P, W], U32, align_bytes=64, name="hq")
-            hs = hqpool.tile([P, W], U8, align_bytes=64, name="hs")
+            hq = hqpool.tile([P, rows_of(i)], U32, align_bytes=64, name="hq")
+            hs = hqpool.tile([P, rows_of(i)], U8, align_bytes=64, name="hs")
             st[("hq", i)] = (hq, hs)
             nc.vector.quantize_mx(out=hq[:].bitcast(FP8X4), scales=hs[:],
                                   in_=st[("hg", i)][:].rearrange("p n t -> p (n t)"))
@@ -223,80 +251,117 @@ def tile_lintrans_pa_t_kernel(tc, x, W1, b1, W2, b2, clusters, out_0, out_1):
                                     lhsT_scale=hs[:, P * blk:P * (blk + 1)],
                                     rhs=w2q[:].bitcast(FP8X4), rhs_scale=w2s[:], start=True, stop=True)
 
-        def layer2_transposed(i, half):
+        def layer2_transposed(i):
             hq, hs = st[("hq", i)]
-            ut = bank([P, W])
-            st[("ut", i, half)] = ut
-            nc.tensor.matmul_mx(out=ut[:], lhsT=w2q[:, P * half:P * (half + 1)].bitcast(FP8X4),
-                                lhsT_scale=w2s[:, P * half:P * (half + 1)],
-                                rhs=hq[:].bitcast(FP8X4), rhs_scale=hs[:], start=True, stop=True)
+            banks = []
+            for half in range(2):
+                ut = side_by_side(i, half)
+                if len(banks) == 0 or SIZES[i] == TB:
+                    banks.append(st["open"])
+                nc.tensor.matmul_mx(out=ut, lhsT=w2q[:, P * half:P * (half + 1)].bitcast(FP8X4),
+                                    lhsT_scale=w2s[:, P * half:P * (half + 1)],
+                                    rhs=hq[:].bitcast(FP8X4), rhs_scale=hs[:], start=True, stop=True)
+            st[("ut", i)] = banks
 
-        def add_b2_and_store(i, pr):
-            if pr == 0:
-                st[("z", i)] = zpool.tile([P, TB, H1], F32, name="zsb")
-            nc.vector.tensor_tensor(out=st[("z", i)][:, 2 * pr:2 * pr + 2, :], in0=st[("up", i, pr)][:],
-                                    in1=b2bc[:].unsqueeze(1).to_broadcast([P, 2, H1]), op=ALU.add)
-            if pr == 1:
-                nc.sync.dma_start(out=z_v[:, TB * i:TB * (i + 1), :], in_=st[("z", i)][:])
+        def add_b2_and_store(i):
+            st[("z", i)] = zpool.tile([P, SIZES[i], H1], F32, name="zsb")
+            for pr in pairs_of(i):
+                nc.vector.tensor_tensor(out=st[("z", i)][:, 2 * pr:2 * pr + 2, :], in0=st[("up", i, pr)][:],
+                                        in1=b2bc[:].unsqueeze(1).to_broadcast([P, 2, H1]), op=ALU.add)
+            nc.sync.dma_start(out=z_v[:, FIRST[i]:FIRST[i + 1], :], in_=st[("z", i)][:])
 
-        def take_hi(i, half):
-            if half == 0:
-                st[("uh", i)] = upool.tile([P, 2, W], BF16, name="uh")
-            nc.scalar.copy(out=st[("uh", i)][:, half, :], in_=st[("ut", i, half)][:])
+        def take_u(i):
+            u0 = upool.tile([P, W], F32, tag="uh", name="u0")
+            u1 = upool.tile([P, W], F32, tag="ul", name="u1")
+            st[("u", i)] = (u0, u1)
+            nc.scalar.copy(out=u0[:], in_=st[("ut", i)][0][:])
+            if i in U_ON_SCALAR:
+                nc.scalar.copy(out=u1[:], in_=st[("ut", i)][1][:])
+            else:
+                nc.vector.tensor_copy(out=u1[:], in_=st[("ut", i)][1][:])
 
-        def take_lo(i, half):
-            if half == 0:
-                st[("ul", i)] = upool.tile([P, 2, W], BF16, name="ul")
-            nc.vector.tensor_tensor(out=st[("ul", i)][:, half, :], in0=st[("ut", i, half)][:],
-                                    in1=st[("uh", i)][:, half, :], op=ALU.subtract)
+        def distances_f32(i):
+            t0, t9 = group_of[i]
+            if i == t0:
+                st[("dg", t0)] = bank([P, W])
+            off = SLOT * (3 - (i - t0))
+            for half in range(2):
+                nc.tensor.matmul(st[("dg", t0)][:], lhsT=wide[:, half, off:off + P], rhs=st[("u", i)][half][:],
+                                 start=(i == t0 and half == 0), stop=(i == t9 - 1 and half == 1))
+
+        def take_distances(t0):
+            dgs = work.tile([P, W], F32, name="dgs")
+            st[("dgs", t0)] = dgs
+            nc.vector.tensor_copy(out=dgs[:], in_=st[("dg", t0)][:])
+
+        def turn_distances(t0):
+            dgs = st[("dgs", t0)]
+            dt = bank([P, TB, P])
+            st[("dt", t0)] = dt
+            for blk in range(TB):
+                nc.tensor.transpose(dt[:, blk, :], dgs[:, P * blk:P * (blk + 1)], ident[:])
+
+        def take_hi(i):
+            uh = upool.tile([P, 2 * rows_of(i)], BF16, tag="uh", name="uh")
+            st[("uh", i)] = uh
+            for r, ut in enumerate(st[("ut", i)]):
+                nc.scalar.copy(out=uh[:, W * r:W * (r + 1)], in_=ut[:])
+
+        def take_lo(i):
+            ul = upool.tile([P, 2 * rows_of(i)], BF16, tag="ul", name="ul")
+            st[("ul", i)] = ul
+            for r, ut in enumerate(st[("ut", i)]):
+                nc.vector.tensor_tensor(out=ul[:, W * r:W * (r + 1)], in0=ut[:],
+                                        in1=st[("uh", i)][:, W * r:W * (r + 1)], op=ALU.subtract)
 
         def sum_squares(i):
-            for blk in range(TB):
+            for blk in range(SIZES[i]):
                 junk = work.tile([P, H1], BF16, name="junk")
                 nc.scalar.activation(out=junk[:], in_=st[("z", i)][:, blk, :], func=ACT.Square,
-                                     accum_out=ssq[:, TB * i + blk:TB * i + blk + 1])
+                                     accum_out=ssq[:, FIRST[i] + blk:FIRST[i] + blk + 1])
 
         def distances(i):
-            dp = bank([P, TB, KC])
+            dp = bank([P, SIZES[i], KC])
             st[("dp", i)] = dp
-            for blk in range(TB):
+            for blk in range(SIZES[i]):
                 for half in range(2):
                     for which, term_of_u in enumerate((st[("uh", i)], st[("ul", i)])):
-                        nc.tensor.matmul(dp[:, blk, :], lhsT=term_of_u[:, half, P * blk:P * (blk + 1)],
-                                         rhs=m2cT[:, half, :], start=(half == 0 and which == 0), stop=False)
-                nc.tensor.matmul(dp[:, blk, :], lhsT=pick[:].to_broadcast([P, P]), rhs=e_rows[:],
-                                 start=False, stop=True)
+                        c0 = rows_of(i) * half + P * blk
+                        nc.tensor.matmul(dp[:, blk, :], lhsT=term_of_u[:, c0:c0 + P],
+                                         rhs=m2cT[:, half, :], start=(half == 0 and which == 0),
+                                         stop=(half == 1 and which == 1))
+
+        def squares_and_e(i):
+            se = sepool.tile([P, SIZES[i], KC], F32, name="se")
+            st[("se", i)] = se
+            nc.gpsimd.tensor_tensor(out=se[:],
+                                    in0=ssq[:, FIRST[i]:FIRST[i + 1]].unsqueeze(2).to_broadcast([P, SIZES[i], KC]),
+                                    in1=e_bc[:].unsqueeze(1).to_broadcast([P, SIZES[i], KC]), op=ALU.add)
 
         def student_t(i):
-            d = den[:, TB * i:TB * (i + 1), :]
-            nc.vector.tensor_tensor(out=d, in0=st[("dp", i)][:],
-                                    in1=ssq[:, TB * i:TB * (i + 1)].unsqueeze(2).to_broadcast([P, TB, KC]),
-                                    op=ALU.add)
+            d = den[:, FIRST[i]:FIRST[i + 1], :]
+            if i in group_of:
+                t0 = group_of[i][0]
+                dist = st[("dt", t0)][:, :, SLOT * (i - t0):SLOT * (i - t0) + KC]
+            else:
+                dist = st[("dp", i)][:]
+            nc.vector.tensor_tensor(out=d, in0=dist, in1=st[("se", i)][:], op=ALU.add)
             nc.vector.reciprocal(out=d, in_=d)
 
-        def normalise_and_store(b0, b9):
+        def normalise_and_store(b0, b9, engine):
             nb = b9 - b0
             d = den[:, b0:b9, :]
             nc.vector.tensor_reduce(out=rsum[:, b0:b9], in_=d, axis=AX.X, op=ALU.add)
             nc.vector.reciprocal(out=rsum[:, b0:b9], in_=rsum[:, b0:b9])
-            nc.vector.tensor_tensor(out=d, in0=d, in1=rsum[:, b0:b9].unsqueeze(2).to_broadcast([P, nb, KC]),
-                                    op=ALU.mult)
+            engine.tensor_tensor(out=d, in0=d, in1=rsum[:, b0:b9].unsqueeze(2).to_broadcast([P, nb, KC]), op=ALU.mult)
             nc.sync.dma_start(out=q_v[:, b0:b9, :], in_=d)
 
-        batch_start = {}
-        for t0, t9 in Q_BATCHES:
-            batch_start[t9 - 1] = t0
-
-        regroup_w1(0)
-        nc.vector.tensor_copy(out=b1col[:], in_=b1raw[:])
-        quantise_w1(0)
-        regroup_w1(1)
-        for s in range(NT + 5 + TRAIL + SQ_LAG):
+        def step(s):
             far = s - 4 - TRAIL
             sq = far - SQ_LAG
-            if s == 4:
+            if s == 7:
                 constants_products()
-            if s == 6:
+            if s == 9:
                 constants_terms()
             if ok(s - 3):
                 regroup_h(s - 3)
@@ -308,45 +373,73 @@ def tile_lintrans_pa_t_kernel(tc, x, W1, b1, W2, b2, clusters, out_0, out_1):
             if ok(s - 1):
                 quantise_x(s - 1)
             if s == 1:
+                quantise_w1(0)
                 quantise_w1(1)
                 regroup_w1(2)
-                regroup_w1(3)
                 quantise_w1(2)
                 quantise_w1(3)
+            if s == 2:
                 regroup_w2()
             if ok(s - 4):
-                layer2_rows(s - 4, 0)
-                layer2_rows(s - 4, 1)
+                for pr in pairs_of(s - 4):
+                    layer2_rows(s - 4, pr)
             if ok(far):
-                layer2_transposed(far, 0)
-                layer2_transposed(far, 1)
+                layer2_transposed(far)
             if ok(s - 3):
                 quantise_h(s - 3)
             if ok(s - 4):
-                add_b2_and_store(s - 4, 0)
-                add_b2_and_store(s - 4, 1)
+                add_b2_and_store(s - 4)
             if ok(sq):
-                distances(sq)
+                if sq in group_of:
+                    distances_f32(sq)
+                    if sq == group_of[sq][1] - 1:
+                        take_distances(group_of[sq][0])
+                else:
+                    distances(sq)
             if ok(far):
-                take_hi(far, 0)
-                take_hi(far, 1)
-                take_lo(far, 0)
-                take_lo(far, 1)
-            if s == 2:
-                quantise_w2()
-                constants_to_f32()
+                if far in group_of:
+                    take_u(far)
+                else:
+                    take_hi(far)
+                    take_lo(far)
             if s == 3:
-                constants_transpose()
+                quantise_w2()
             if s == 5:
+                constants_to_f32()
+            if s == 6:
+                constants_transpose()
+            if s == 8:
                 constants_sum()
             if ok(s):
                 transpose_x(s)
             if ok(sq - 1):
-                student_t(sq - 1)
-                if (sq - 1) in batch_start:
-                    normalise_and_store(TB * batch_start[sq - 1], TB * sq)
+                if (sq - 1) not in group_of:
+                    student_t(sq - 1)
+                elif sq == group_of[sq - 1][1]:
+                    turn_distances(group_of[sq - 1][0])
+            if (sq - 2) in group_of and sq - 1 == group_of[sq - 2][1]:
+                for i in range(group_of[sq - 2][0], sq - 1):
+                    student_t(i)
+            for t0, t9 in Q_BATCHES:
+                if sq - 1 == (t9 if t9 - 1 in group_of else t9 - 1):
+                    normalise_and_store(FIRST[t0], FIRST[t9], nc.gpsimd if t9 < NT - 3 else nc.vector)
             if ok(sq):
                 sum_squares(sq)
+                squares_and_e(sq)
             if ok(s):
-                copy_x(s, 0)
-                copy_x(s, 1)
+                for pr in pairs_of(s):
+                    copy_x(s, pr)
+            if s == 0:
+                regroup_w1(0)
+                regroup_w1(1)
+                regroup_w1(3)
+
+        with tc.manual_schedule(engines={mybir.EngineType.PE, mybir.EngineType.Activation, mybir.EngineType.DVE}):
+            idle = bank([P, 2 * P])
+            for r in range(WARM_UP):
+                nc.tensor.matmul(idle[:], lhsT=zeros[:, 0:P], rhs=zeros[:], start=True, stop=True)
+            nc.vector.tensor_copy(out=b1col[:], in_=b1raw[:])
+            for s in range(HEAD):
+                step(s)
+        for s in range(HEAD, NT + 5 + TRAIL + SQ_LAG):
+            step(s)

@@ -24,11 +24,13 @@ PSUM_BANKS = 8
 
 TRAIL = 4
 SQ_LAG = 2
-X_COPY_ON_VECTOR = []
+X_COPY_ON_VECTOR = [3, 4, 5, 7, 8, 10, 11, 13, 14]
 F32_GROUPS = [(2, 6), (6, 10)]
-U_ON_SCALAR = [3, 5, 7]
 SLOT = 32
-Q_BATCHES = [(0, 6), (6, 10), (10, 13), (13, 15), (15, 16), (16, 17), (17, 18)]
+Q_BATCHES = [(0, 5, 10), (5, 10, 11), (10, 13, 12), (13, 15, 14), (15, 16, 15), (16, 17, 16), (17, 18, 17)]
+T_ON_SCALAR = 15
+T_BATCHES = {10: (0, 10), 12: (10, 13), 14: (13, 15)}
+HI_ON_VECTOR = range(11, 16)
 
 WARM_UP = 6
 HEAD = 3
@@ -275,10 +277,7 @@ def tile_lintrans_pa_t_kernel(tc, x, W1, b1, W2, b2, clusters, out_0, out_1):
             u1 = upool.tile([P, W], F32, tag="ul", name="u1")
             st[("u", i)] = (u0, u1)
             nc.scalar.copy(out=u0[:], in_=st[("ut", i)][0][:])
-            if i in U_ON_SCALAR:
-                nc.scalar.copy(out=u1[:], in_=st[("ut", i)][1][:])
-            else:
-                nc.vector.tensor_copy(out=u1[:], in_=st[("ut", i)][1][:])
+            nc.vector.tensor_copy(out=u1[:], in_=st[("ut", i)][1][:])
 
         def distances_f32(i):
             t0, t9 = group_of[i]
@@ -305,7 +304,10 @@ def tile_lintrans_pa_t_kernel(tc, x, W1, b1, W2, b2, clusters, out_0, out_1):
             uh = upool.tile([P, 2 * rows_of(i)], BF16, tag="uh", name="uh")
             st[("uh", i)] = uh
             for r, ut in enumerate(st[("ut", i)]):
-                nc.scalar.copy(out=uh[:, W * r:W * (r + 1)], in_=ut[:])
+                if r == 1 and i in HI_ON_VECTOR:
+                    nc.vector.tensor_copy(out=uh[:, W * r:W * (r + 1)], in_=ut[:])
+                else:
+                    nc.scalar.copy(out=uh[:, W * r:W * (r + 1)], in_=ut[:])
 
         def take_lo(i):
             ul = upool.tile([P, 2 * rows_of(i)], BF16, tag="ul", name="ul")
@@ -346,7 +348,13 @@ def tile_lintrans_pa_t_kernel(tc, x, W1, b1, W2, b2, clusters, out_0, out_1):
             else:
                 dist = st[("dp", i)][:]
             nc.vector.tensor_tensor(out=d, in0=dist, in1=st[("se", i)][:], op=ALU.add)
-            nc.vector.reciprocal(out=d, in_=d)
+            if i >= T_ON_SCALAR:
+                nc.vector.reciprocal(out=d, in_=d)
+
+        def batch_t(b0, b9):
+            d = den[:, b0:b9, :]
+            nc.scalar.activation(out=d, in_=d, func=ACT.Abs_reciprocal_sqrt)
+            nc.scalar.activation(out=d, in_=d, func=ACT.Square)
 
         def normalise_and_store(b0, b9, engine):
             nb = b9 - b0
@@ -420,9 +428,12 @@ def tile_lintrans_pa_t_kernel(tc, x, W1, b1, W2, b2, clusters, out_0, out_1):
             if (sq - 2) in group_of and sq - 1 == group_of[sq - 2][1]:
                 for i in range(group_of[sq - 2][0], sq - 1):
                     student_t(i)
-            for t0, t9 in Q_BATCHES:
-                if sq - 1 == (t9 if t9 - 1 in group_of else t9 - 1):
-                    normalise_and_store(FIRST[t0], FIRST[t9], nc.gpsimd if t9 < NT - 3 else nc.vector)
+            if (sq - 1) in T_BATCHES:
+                t0, t9 = T_BATCHES[sq - 1]
+                batch_t(FIRST[t0], FIRST[t9])
+            for t0, t9, last in Q_BATCHES:
+                if sq - 1 == last:
+                    normalise_and_store(FIRST[t0], FIRST[t9], nc.gpsimd if t9 <= 10 else nc.vector)
             if ok(sq):
                 sum_squares(sq)
                 squares_and_e(sq)

@@ -24,13 +24,13 @@ PSUM_BANKS = 8
 
 TRAIL = 4
 SQ_LAG = 2
-X_COPY_ON_VECTOR = [3, 4, 5, 7, 8, 10, 11, 13, 14]
+X_COPY_ON_VECTOR = [3, 4, 5, 6, 7, 8, 10, 11, 12, 13, 14]
 F32_GROUPS = [(2, 6), (6, 10)]
 SLOT = 32
-Q_BATCHES = [(0, 5, 10), (5, 10, 11), (10, 13, 12), (13, 15, 14), (15, 16, 15), (16, 17, 16), (17, 18, 17)]
-T_ON_SCALAR = 15
-T_BATCHES = {10: (0, 10), 12: (10, 13), 14: (13, 15)}
-HI_ON_VECTOR = range(11, 16)
+Q_BATCHES = [(0, 5, 10), (5, 10, 11), (10, 13, 12), (13, 16, 15), (16, 18, 17)]
+T_ON_SCALAR = 16
+T_BATCHES = {10: (0, 10), 12: (10, 13), 15: (13, 16)}
+HI_ON_VECTOR = range(13, 16)
 
 WARM_UP = 6
 HEAD = 3
@@ -381,9 +381,8 @@ def tile_lintrans_pa_t_kernel(tc, x, W1, b1, W2, b2, clusters, out_0, out_1):
             if ok(s - 1):
                 quantise_x(s - 1)
             if s == 1:
-                quantise_w1(0)
-                quantise_w1(1)
                 regroup_w1(2)
+                quantise_w1(1)
                 quantise_w1(2)
                 quantise_w1(3)
             if s == 2:
@@ -442,6 +441,8 @@ def tile_lintrans_pa_t_kernel(tc, x, W1, b1, W2, b2, clusters, out_0, out_1):
                     copy_x(s, pr)
             if s == 0:
                 regroup_w1(0)
+                nc.vector.tensor_copy(out=b1col[:], in_=b1raw[:])
+                quantise_w1(0)
                 regroup_w1(1)
                 regroup_w1(3)
 
@@ -449,7 +450,6 @@ def tile_lintrans_pa_t_kernel(tc, x, W1, b1, W2, b2, clusters, out_0, out_1):
             idle = bank([P, 2 * P])
             for r in range(WARM_UP):
                 nc.tensor.matmul(idle[:], lhsT=zeros[:, 0:P], rhs=zeros[:], start=True, stop=True)
-            nc.vector.tensor_copy(out=b1col[:], in_=b1raw[:])
             for s in range(HEAD):
                 step(s)
         for s in range(HEAD, NT + 5 + TRAIL + SQ_LAG):

@@ -110,7 +110,7 @@ def tile_lintrans_pa_t_kernel(tc, x, W1, b1, W2, b2, clusters, out_0, out_1):
         w2q = keep.tile([P, H1], U32, align_bytes=64)
         w2s = keep.tile([P, H1], U8, align_bytes=64)
         m2cT = keep.tile([P, 2, KC], BF16)
-        e_bc = keep.tile([P, KC], F32)
+        e_bc = keep.tile([P, KC + 1], F32)
         ssq = keep.tile([P, NB], F32)
         den = keep.tile([P, NB, KC], F32)
         rsum = keep.tile([P, NB], F32)
@@ -138,7 +138,9 @@ def tile_lintrans_pa_t_kernel(tc, x, W1, b1, W2, b2, clusters, out_0, out_1):
 
         parf = keep.tile([P, P], F32)
         cst = keep.tile([P, P], F32)
-        cw = keep.tile([P, 2, KC], F32)
+        cd = keep.tile([P, 2, KC], F32)
+        cw = keep.tile([P, 2, P], F32)
+        nc.gpsimd.memset(cw[:], 0.0)
 
         def constants_to_f32():
             nc.gpsimd.tensor_copy(out=parf[:], in_=par[:])
@@ -156,14 +158,22 @@ def tile_lintrans_pa_t_kernel(tc, x, W1, b1, W2, b2, clusters, out_0, out_1):
             b2x2 = keep.tile([P, 2], F32)
             nc.vector.tensor_scalar(out=b2x2[:], in0=cst[:, 64:66], scalar1=2.0, scalar2=None, op0=ALU.mult)
             for half in range(2):
-                nc.vector.tensor_scalar(out=cw[:, half, :], in0=cT[:, half, :], scalar1=b2x2[:, half:half + 1],
+                nc.vector.tensor_scalar(out=cd[:, half, :], in0=cT[:, half, :], scalar1=b2x2[:, half:half + 1],
                                         scalar2=None, op0=ALU.subtract)
-            nc.vector.tensor_tensor(out=cw[:], in0=cw[:], in1=cT, op=ALU.mult)
+            per_slot = [P, 2, P // SLOT, KC]
+            nc.vector.tensor_tensor(out=cw[:].rearrange("p h (s k) -> p h s k", k=SLOT)[:, :, :, 0:KC],
+                                    in0=cd[:].unsqueeze(2).to_broadcast(per_slot),
+                                    in1=cT.unsqueeze(2).to_broadcast(per_slot), op=ALU.mult)
 
         def constants_sum():
-            st["e_ps"] = bank([P, KC])
+            e_ps = bank([P, KC + 1])
+            st["e_ps"] = e_ps
             for half in range(2):
-                nc.tensor.matmul(st["e_ps"][:], lhsT=ones[:], rhs=cw[:, half, :], start=(half == 0), stop=(half == 1))
+                nc.tensor.matmul(e_ps[:, 0:KC], lhsT=ones[:], rhs=cw[:, half, 0:KC], start=(half == 0),
+                                 stop=(half == 1))
+            for half in range(2):
+                nc.tensor.matmul(e_ps[:, KC:KC + 1], lhsT=cw[:, half, :], rhs=ones[:, 0:1], start=(half == 0),
+                                 stop=(half == 1))
 
         def constants_terms():
             nc.vector.tensor_scalar(out=e_bc[:], in0=st["e_ps"][:], scalar1=1.0, scalar2=None, op0=ALU.add)
@@ -291,7 +301,8 @@ def tile_lintrans_pa_t_kernel(tc, x, W1, b1, W2, b2, clusters, out_0, out_1):
         def take_distances(t0):
             dgs = work.tile([P, W], F32, name="dgs")
             st[("dgs", t0)] = dgs
-            nc.vector.tensor_copy(out=dgs[:], in_=st[("dg", t0)][:])
+            nc.vector.tensor_scalar(out=dgs[:], in0=st[("dg", t0)][:], scalar1=e_bc[:, KC:KC + 1], scalar2=None,
+                                    op0=ALU.add)
 
         def turn_distances(t0):
             dgs = st[("dgs", t0)]
@@ -338,18 +349,22 @@ def tile_lintrans_pa_t_kernel(tc, x, W1, b1, W2, b2, clusters, out_0, out_1):
             st[("se", i)] = se
             nc.gpsimd.tensor_tensor(out=se[:],
                                     in0=ssq[:, FIRST[i]:FIRST[i + 1]].unsqueeze(2).to_broadcast([P, SIZES[i], KC]),
-                                    in1=e_bc[:].unsqueeze(1).to_broadcast([P, SIZES[i], KC]), op=ALU.add)
+                                    in1=e_bc[:, 0:KC].unsqueeze(1).to_broadcast([P, SIZES[i], KC]), op=ALU.add)
 
         def student_t(i):
             d = den[:, FIRST[i]:FIRST[i + 1], :]
-            if i in group_of:
-                t0 = group_of[i][0]
-                dist = st[("dt", t0)][:, :, SLOT * (i - t0):SLOT * (i - t0) + KC]
-            else:
-                dist = st[("dp", i)][:]
-            nc.vector.tensor_tensor(out=d, in0=dist, in1=st[("se", i)][:], op=ALU.add)
+            nc.vector.tensor_tensor(out=d, in0=st[("dp", i)][:], in1=st[("se", i)][:], op=ALU.add)
             if i >= T_ON_SCALAR:
                 nc.vector.reciprocal(out=d, in_=d)
+
+        def group_distances(t0):
+            t9 = group_of[t0][1]
+            n = t9 - t0
+            nc.vector.tensor_tensor(
+                out=den[:, FIRST[t0]:FIRST[t9], :].rearrange("p (s b) k -> p s b k", b=TB),
+                in0=st[("dt", t0)][:].rearrange("p b (s k) -> p s b k", k=SLOT)[:, 0:n, :, 0:KC],
+                in1=ssq[:, FIRST[t0]:FIRST[t9]].rearrange("p (s b) -> p s b", b=TB).unsqueeze(3).to_broadcast([P, n, TB, KC]),
+                op=ALU.add)
 
         def batch_t(b0, b9):
             d = den[:, b0:b9, :]
@@ -425,8 +440,7 @@ def tile_lintrans_pa_t_kernel(tc, x, W1, b1, W2, b2, clusters, out_0, out_1):
                 elif sq == group_of[sq - 1][1]:
                     turn_distances(group_of[sq - 1][0])
             if (sq - 2) in group_of and sq - 1 == group_of[sq - 2][1]:
-                for i in range(group_of[sq - 2][0], sq - 1):
-                    student_t(i)
+                group_distances(group_of[sq - 2][0])
             if (sq - 1) in T_BATCHES:
                 t0, t9 = T_BATCHES[sq - 1]
                 batch_t(FIRST[t0], FIRST[t9])
@@ -435,7 +449,8 @@ def tile_lintrans_pa_t_kernel(tc, x, W1, b1, W2, b2, clusters, out_0, out_1):
                     normalise_and_store(FIRST[t0], FIRST[t9], nc.gpsimd if t9 <= 10 else nc.vector)
             if ok(sq):
                 sum_squares(sq)
-                squares_and_e(sq)
+                if sq not in group_of:
+                    squares_and_e(sq)
             if ok(s):
                 for pr in pairs_of(s):
                     copy_x(s, pr)

from contextlib import ExitStack

from concourse import mybir
from concourse.masks import make_identity

F32 = mybir.dt.float32
BF16 = mybir.dt.bfloat16
U32 = mybir.dt.uint32
U8 = mybir.dt.uint8
FP8X4 = mybir.dt.float8_e4m3fn_x4
ACT = mybir.ActivationFunctionType
ALU = mybir.AluOpType
AX = mybir.AxisListType

P = 128
N_ROWS, D_IN, H0, H1, KC = 8192, 512, 512, 256, 20
NB = N_ROWS // P
TB = 4
W = TB * P
SIZES = [2, 2] + [TB] * 14 + [2, 2]
NT = len(SIZES)
FIRST = [sum(SIZES[:i]) for i in range(NT + 1)]
PSUM_BANKS = 8

TRAIL = 4
SQ_LAG = 2
X_COPY_ON_VECTOR = [3, 4, 5, 6, 7, 8, 10, 11, 12, 13, 14]
F32_GROUPS = [(2, 6), (6, 10)]
SLOT = 32
Q_BATCHES = [(0, 5, 10), (5, 10, 11), (10, 13, 12), (13, 16, 15), (16, 18, 17)]
T_ON_SCALAR = 16
T_BATCHES = {10: (0, 10), 12: (10, 13), 15: (13, 16)}
HI_ON_VECTOR = range(13, 16)

WARM_UP = 6
HEAD = 3

FLOPS = 2 * N_ROWS * (D_IN * H0 + H0 * H1 + H1 * KC)


def tile_lintrans_pa_t_kernel(tc, x, W1, b1, W2, b2, clusters, out_0, out_1):
    nc = tc.nc
    x_v = x.rearrange("(p b) k -> p b k", b=NB)
    z_v = out_0.rearrange("(p b) j -> p b j", b=NB)
    q_v = out_1.rearrange("(p b) k -> p b k", b=NB)

    with ExitStack() as es:
        keep = es.enter_context(tc.tile_pool(name="keep", bufs=1))
        xin_pool = es.enter_context(tc.tile_pool(name="xin", bufs=NT))
        work = es.enter_context(tc.tile_pool(name="work", bufs=3))
        work3 = es.enter_context(tc.tile_pool(name="work3", bufs=3))
        zpool = es.enter_context(tc.tile_pool(name="zpool", bufs=TRAIL + SQ_LAG + 4))
        upool = es.enter_context(tc.tile_pool(name="upool", bufs=SQ_LAG + 3))
        hqpool = es.enter_context(tc.tile_pool(name="hqpool", bufs=TRAIL + 3))
        sepool = es.enter_context(tc.tile_pool(name="sepool", bufs=6))
        psum = es.enter_context(tc.psum_pool(name="psum", bufs=PSUM_BANKS))

        def bank(shape):
            return psum.tile(shape, F32, tag="bank", name="bank")

        zeros = keep.tile([P, 2 * P], BF16)
        nc.vector.memset(zeros[:], 0.0)

        ident = keep.tile([P, P], F32)
        make_identity(nc, ident[:])

        xin = []

        def load_x(i):
            rows = xin_pool.tile([P, SIZES[i], D_IN], BF16, name="xin")
            nc.sync.dma_start(out=rows[:], in_=x_v[:, FIRST[i]:FIRST[i + 1], :])
            xin.append(rows)

        load_x(0)
        w1raw = keep.tile([P, 4, H0], BF16)
        for u in range(2):
            nc.sync.dma_start(
                out=w1raw[:, 2 * u:2 * u + 2, :],
                in_=W1[256 * u:256 * (u + 1), :].rearrange("(q e) c -> q e c", e=2),
            )
        b1raw = keep.tile([P, 4], BF16)
        nc.scalar.dma_start(out=b1raw[:], in_=b1.rearrange("(p m) -> p m", m=4))
        warm = keep.tile([P, 1], F32)
        nc.vector.memset(warm[:], 0.0)
        nc.scalar.activation(out=warm[:], in_=warm[:], func=ACT.Silu)
        par = keep.tile([P, P], BF16)
        nc.gpsimd.memset(par[:], 0.0)
        nc.gpsimd.dma_start(out=par[0:KC, :], in_=clusters[:, 0:P])
        nc.gpsimd.dma_start(out=par[32:32 + KC, :], in_=clusters[:, P:2 * P])
        nc.gpsimd.dma_start(out=par[64:66, :], in_=b2.rearrange("(half j) -> half j", j=P))
        load_x(1)
        load_x(2)
        w2raw = keep.tile([P, 4, H1], BF16)
        nc.sync.dma_start(out=w2raw[:], in_=W2.rearrange("(p m) j -> p m j", m=4))
        b2bc = keep.tile([P, H1], BF16)
        nc.sync.dma_start(out=b2bc[:], in_=b2.partition_broadcast(P))
        for i in range(3, NT):
            load_x(i)

        ones = keep.tile([P, P], F32)
        nc.gpsimd.memset(ones[:], 1.0)
        wide = keep.tile([P, 2, P + 3 * SLOT], F32)
        nc.gpsimd.memset(wide[:], 0.0)

        w1g = keep.tile([P, H0, 4], BF16, align_bytes=64)
        w1q = keep.tile([P, H0], U32, align_bytes=64)
        w1s = keep.tile([P, H0], U8, align_bytes=64)
        b1col = keep.tile([P, 4], F32)
        w2g = keep.tile([P, H1, 4], BF16, align_bytes=64)
        w2q = keep.tile([P, H1], U32, align_bytes=64)
        w2s = keep.tile([P, H1], U8, align_bytes=64)
        m2cT = keep.tile([P, 2, KC], BF16)
        e_bc = keep.tile([P, KC + 1], F32)
        ssq = keep.tile([P, NB], F32)
        den = keep.tile([P, NB, KC], F32)
        rsum = keep.tile([P, NB], F32)

        def regroup_w1(m):
            part = w1g[:, P * m:P * (m + 1), :]
            raw = w1raw[:].rearrange("q t (p m) -> q m p t", m=4)[:, m]
            if m % 2:
                nc.scalar.copy(out=part, in_=raw)
            else:
                nc.vector.tensor_copy(out=part, in_=raw)

        def quantise_w1(m):
            nc.vector.quantize_mx(out=w1q[:, P * m:P * (m + 1)].bitcast(FP8X4), scales=w1s[:, P * m:P * (m + 1)],
                                  in_=w1g[:, P * m:P * (m + 1), :].rearrange("q c t -> q (c t)"))

        st = {}

        def regroup_w2():
            nc.vector.tensor_copy(out=w2g[:], in_=w2raw[:].rearrange("p m j -> p j m"))

        def quantise_w2():
            nc.vector.quantize_mx(out=w2q[:].bitcast(FP8X4), scales=w2s[:],
                                  in_=w2g[:].rearrange("p j m -> p (j m)"))

        parf = keep.tile([P, P], F32)
        cst = keep.tile([P, P], F32)
        cd = keep.tile([P, 2, KC], F32)
        cw = keep.tile([P, 2, P], F32)
        nc.gpsimd.memset(cw[:], 0.0)

        def constants_to_f32():
            nc.gpsimd.tensor_copy(out=parf[:], in_=par[:])

        def constants_transpose():
            st["par_ps"] = bank([P, P])
            nc.tensor.transpose(st["par_ps"][:], parf[:], ident[:])

        def constants_products():
            nc.vector.tensor_copy(out=cst[:], in_=st["par_ps"][:])
            cT = cst[:, 0:64].rearrange("p (half k) -> p half k", half=2)[:, :, 0:KC]
            nc.vector.tensor_scalar(out=m2cT[:], in0=cT, scalar1=-2.0, scalar2=None, op0=ALU.mult)
            nc.vector.tensor_scalar(out=wide[:, :, 3 * SLOT:3 * SLOT + KC], in0=cT, scalar1=-2.0, scalar2=None,
                                    op0=ALU.mult)
            b2x2 = keep.tile([P, 2], F32)
            nc.vector.tensor_scalar(out=b2x2[:], in0=cst[:, 64:66], scalar1=2.0, scalar2=None, op0=ALU.mult)
            for half in range(2):
                nc.vector.tensor_scalar(out=cd[:, half, :], in0=cT[:, half, :], scalar1=b2x2[:, half:half + 1],
                                        scalar2=None, op0=ALU.subtract)
            per_slot = [P, 2, P // SLOT, KC]
            nc.vector.tensor_tensor(out=cw[:].rearrange("p h (s k) -> p h s k", k=SLOT)[:, :, :, 0:KC],
                                    in0=cd[:].unsqueeze(2).to_broadcast(per_slot),
                                    in1=cT.unsqueeze(2).to_broadcast(per_slot), op=ALU.mult)

        def constants_sum():
            e_ps = bank([P, KC + 1])
            st["e_ps"] = e_ps
            for half in range(2):
                nc.tensor.matmul(e_ps[:, 0:KC], lhsT=ones[:], rhs=cw[:, half, 0:KC], start=(half == 0),
                                 stop=(half == 1))
            for half in range(2):
                nc.tensor.matmul(e_ps[:, KC:KC + 1], lhsT=cw[:, half, :], rhs=ones[:, 0:1], start=(half == 0),
                                 stop=(half == 1))

        def constants_terms():
            nc.vector.tensor_scalar(out=e_bc[:], in0=st["e_ps"][:], scalar1=1.0, scalar2=None, op0=ALU.add)

        group_of = {}
        for t0, t9 in F32_GROUPS:
            for i in range(t0, t9):
                group_of[i] = (t0, t9)

        def ok(i):
            return 0 <= i < NT

        def rows_of(i):
            return P * SIZES[i]

        def pairs_of(i):
            return range(SIZES[i] // 2)

        def side_by_side(i, r):
            n = rows_of(i)
            per = W // n
            if r % per == 0:
                st["open"] = bank([P, W])
            return st["open"][:, n * (r % per):n * (r % per + 1)]

        def transpose_x(i):
            xf = xin[i][:].bitcast(F32)
            for pr in pairs_of(i):
                xt = bank([P, 2, 2, P])
                st[("xt", i, pr)] = xt
                for bb in range(2):
                    for u in range(2):
                        nc.tensor.transpose(xt[:, bb, u, :], xf[:, 2 * pr + bb, P * u:P * (u + 1)], ident[:])

        def copy_x(i, pr):
            if pr == 0:
                xg = work.tile([P, rows_of(i) * 4], BF16, align_bytes=64, name="xg")
                st[("xg", i)] = xg
            xg = st[("xg", i)]
            xgf = xg[:].bitcast(F32).rearrange("p (b n u) -> p b n u", b=SIZES[i], u=2)
            src = st[("xt", i, pr)][:].rearrange("p b u n -> p b n u")
            if pr == 0 and i in X_COPY_ON_VECTOR:
                nc.vector.tensor_copy(out=xgf[:, 2 * pr:2 * pr + 2, :, :], in_=src)
            else:
                nc.scalar.copy(out=xgf[:, 2 * pr:2 * pr + 2, :, :], in_=src)

        def quantise_x(i):
            xq = work3.tile([P, rows_of(i)], U32, align_bytes=64, name="xq")
            xs = work3.tile([P, rows_of(i)], U8, align_bytes=64, name="xs")
            st[("xq", i)] = (xq, xs)
            nc.vector.quantize_mx(out=xq[:].bitcast(FP8X4), scales=xs[:], in_=st[("xg", i)][:])

        def layer1(i, m):
            xq, xs = st[("xq", i)]
            hp = side_by_side(i, m)
            st[("hp", i, m)] = hp
            nc.tensor.matmul_mx(out=hp, lhsT=w1q[:, P * m:P * (m + 1)].bitcast(FP8X4),
                                lhsT_scale=w1s[:, P * m:P * (m + 1)],
                                rhs=xq[:].bitcast(FP8X4), rhs_scale=xs[:], start=True, stop=True)

        def silu(i, m):
            if m == 0:
                st[("hb", i)] = work.tile([P, 4, rows_of(i)], BF16, name="hb")
            nc.scalar.activation(out=st[("hb", i)][:, m, :], in_=st[("hp", i, m)], func=ACT.Silu,
                                 bias=b1col[:, m:m + 1], scale=1.0)

        def regroup_h(i):
            hg = work.tile([P, rows_of(i), 4], BF16, align_bytes=64, name="hg")
            st[("hg", i)] = hg
            nc.vector.tensor_copy(out=hg[:].rearrange("p (c i) t -> p c t i", i=4),
                                  in_=st[("hb", i)][:].rearrange("p t (c i) -> p c t i", i=4))

        def quantise_h(i):
            hq = hqpool.tile([P, rows_of(i)], U32, align_bytes=64, name="hq")
            hs = hqpool.tile([P, rows_of(i)], U8, align_bytes=64, name="hs")
            st[("hq", i)] = (hq, hs)
            nc.vector.quantize_mx(out=hq[:].bitcast(FP8X4), scales=hs[:],
                                  in_=st[("hg", i)][:].rearrange("p n t -> p (n t)"))

        def layer2_rows(i, pr):
            hq, hs = st[("hq", i)]
            up = bank([P, 2, H1])
            st[("up", i, pr)] = up
            for bb in range(2):
                blk = 2 * pr + bb
                nc.tensor.matmul_mx(out=up[:, bb, :], lhsT=hq[:, P * blk:P * (blk + 1)].bitcast(FP8X4),
                                    lhsT_scale=hs[:, P * blk:P * (blk + 1)],
                                    rhs=w2q[:].bitcast(FP8X4), rhs_scale=w2s[:], start=True, stop=True)

        def layer2_transposed(i):
            hq, hs = st[("hq", i)]
            banks = []
            for half in range(2):
                ut = side_by_side(i, half)
                if len(banks) == 0 or SIZES[i] == TB:
                    banks.append(st["open"])
                nc.tensor.matmul_mx(out=ut, lhsT=w2q[:, P * half:P * (half + 1)].bitcast(FP8X4),
                                    lhsT_scale=w2s[:, P * half:P * (half + 1)],
                                    rhs=hq[:].bitcast(FP8X4), rhs_scale=hs[:], start=True, stop=True)
            st[("ut", i)] = banks

        def add_b2_and_store(i):
            st[("z", i)] = zpool.tile([P, SIZES[i], H1], F32, name="zsb")
            for pr in pairs_of(i):
                nc.vector.tensor_tensor(out=st[("z", i)][:, 2 * pr:2 * pr + 2, :], in0=st[("up", i, pr)][:],
                                        in1=b2bc[:].unsqueeze(1).to_broadcast([P, 2, H1]), op=ALU.add)
            nc.sync.dma_start(out=z_v[:, FIRST[i]:FIRST[i + 1], :], in_=st[("z", i)][:])

        def take_u(i):
            u0 = upool.tile([P, W], F32, tag="uh", name="u0")
            u1 = upool.tile([P, W], F32, tag="ul", name="u1")
            st[("u", i)] = (u0, u1)
            nc.scalar.copy(out=u0[:], in_=st[("ut", i)][0][:])
            nc.vector.tensor_copy(out=u1[:], in_=st[("ut", i)][1][:])

        def distances_f32(i):
            t0, t9 = group_of[i]
            if i == t0:
                st[("dg", t0)] = bank([P, W])
            off = SLOT * (3 - (i - t0))
            for half in range(2):
                nc.tensor.matmul(st[("dg", t0)][:], lhsT=wide[:, half, off:off + P], rhs=st[("u", i)][half][:],
                                 start=(i == t0 and half == 0), stop=(i == t9 - 1 and half == 1))

        def take_distances(t0):
            dgs = work.tile([P, W], F32, name="dgs")
            st[("dgs", t0)] = dgs
            nc.vector.tensor_scalar(out=dgs[:], in0=st[("dg", t0)][:], scalar1=e_bc[:, KC:KC + 1], scalar2=None,
                                    op0=ALU.add)

        def turn_distances(t0):
            dgs = st[("dgs", t0)]
            dt = bank([P, TB, P])
            st[("dt", t0)] = dt
            for blk in range(TB):
                nc.tensor.transpose(dt[:, blk, :], dgs[:, P * blk:P * (blk + 1)], ident[:])

        def take_hi(i):
            uh = upool.tile([P, 2 * rows_of(i)], BF16, tag="uh", name="uh")
            st[("uh", i)] = uh
            for r, ut in enumerate(st[("ut", i)]):
                if r == 1 and i in HI_ON_VECTOR:
                    nc.vector.tensor_copy(out=uh[:, W * r:W * (r + 1)], in_=ut[:])
                else:
                    nc.scalar.copy(out=uh[:, W * r:W * (r + 1)], in_=ut[:])

        def take_lo(i):
            ul = upool.tile([P, 2 * rows_of(i)], BF16, tag="ul", name="ul")
            st[("ul", i)] = ul
            for r, ut in enumerate(st[("ut", i)]):
                nc.vector.tensor_tensor(out=ul[:, W * r:W * (r + 1)], in0=ut[:],
                                        in1=st[("uh", i)][:, W * r:W * (r + 1)], op=ALU.subtract)

        def sum_squares(i):
            for blk in range(SIZES[i]):
                junk = work.tile([P, H1], BF16, name="junk")
                nc.scalar.activation(out=junk[:], in_=st[("z", i)][:, blk, :], func=ACT.Square,
                                     accum_out=ssq[:, FIRST[i] + blk:FIRST[i] + blk + 1])

        def distances(i):
            dp = bank([P, SIZES[i], KC])
            st[("dp", i)] = dp
            for blk in range(SIZES[i]):
                for half in range(2):
                    for which, term_of_u in enumerate((st[("uh", i)], st[("ul", i)])):
                        c0 = rows_of(i) * half + P * blk
                        nc.tensor.matmul(dp[:, blk, :], lhsT=term_of_u[:, c0:c0 + P],
                                         rhs=m2cT[:, half, :], start=(half == 0 and which == 0),
                                         stop=(half == 1 and which == 1))

        def squares_and_e(i):
            se = sepool.tile([P, SIZES[i], KC], F32, name="se")
            st[("se", i)] = se
            nc.gpsimd.tensor_tensor(out=se[:],
                                    in0=ssq[:, FIRST[i]:FIRST[i + 1]].unsqueeze(2).to_broadcast([P, SIZES[i], KC]),
                                    in1=e_bc[:, 0:KC].unsqueeze(1).to_broadcast([P, SIZES[i], KC]), op=ALU.add)

        def student_t(i):
            d = den[:, FIRST[i]:FIRST[i + 1], :]
            nc.vector.tensor_tensor(out=d, in0=st[("dp", i)][:], in1=st[("se", i)][:], op=ALU.add)
            if i >= T_ON_SCALAR:
                nc.vector.reciprocal(out=d, in_=d)

        def group_distances(t0):
            t9 = group_of[t0][1]
            n = t9 - t0
            nc.vector.tensor_tensor(
                out=den[:, FIRST[t0]:FIRST[t9], :].rearrange("p (s b) k -> p s b k", b=TB),
                in0=st[("dt", t0)][:].rearrange("p b (s k) -> p s b k", k=SLOT)[:, 0:n, :, 0:KC],
                in1=ssq[:, FIRST[t0]:FIRST[t9]].rearrange("p (s b) -> p s b", b=TB).unsqueeze(3).to_broadcast([P, n, TB, KC]),
                op=ALU.add)

        def batch_t(b0, b9):
            d = den[:, b0:b9, :]
            nc.scalar.activation(out=d, in_=d, func=ACT.Abs_reciprocal_sqrt)
            nc.scalar.activation(out=d, in_=d, func=ACT.Square)

        def normalise_and_store(b0, b9, engine):
            nb = b9 - b0
            d = den[:, b0:b9, :]
            nc.vector.tensor_reduce(out=rsum[:, b0:b9], in_=d, axis=AX.X, op=ALU.add)
            nc.vector.reciprocal(out=rsum[:, b0:b9], in_=rsum[:, b0:b9])
            engine.tensor_tensor(out=d, in0=d, in1=rsum[:, b0:b9].unsqueeze(2).to_broadcast([P, nb, KC]), op=ALU.mult)
            nc.sync.dma_start(out=q_v[:, b0:b9, :], in_=d)

        def step(s):
            far = s - 4 - TRAIL
            sq = far - SQ_LAG
            if s == 7:
                constants_products()
            if s == 9:
                constants_terms()
            if ok(s - 3):
                regroup_h(s - 3)
            if ok(s - 2):
                for m in range(4):
                    layer1(s - 2, m)
                for m in range(4):
                    silu(s - 2, m)
            if ok(s - 1):
                quantise_x(s - 1)
            if s == 1:
                regroup_w1(2)
                quantise_w1(1)
                quantise_w1(2)
                quantise_w1(3)
            if s == 2:
                regroup_w2()
            if ok(s - 4):
                for pr in pairs_of(s - 4):
                    layer2_rows(s - 4, pr)
            if ok(far):
                layer2_transposed(far)
            if ok(s - 3):
                quantise_h(s - 3)
            if ok(s - 4):
                add_b2_and_store(s - 4)
            if ok(sq):
                if sq in group_of:
                    distances_f32(sq)
                    if sq == group_of[sq][1] - 1:
                        take_distances(group_of[sq][0])
                else:
                    distances(sq)
            if ok(far):
                if far in group_of:
                    take_u(far)
                else:
                    take_hi(far)
                    take_lo(far)
            if s == 3:
                quantise_w2()
            if s == 5:
                constants_to_f32()
            if s == 6:
                constants_transpose()
            if s == 8:
                constants_sum()
            if ok(s):
                transpose_x(s)
            if ok(sq - 1):
                if (sq - 1) not in group_of:
                    student_t(sq - 1)
                elif sq == group_of[sq - 1][1]:
                    turn_distances(group_of[sq - 1][0])
            if (sq - 2) in group_of and sq - 1 == group_of[sq - 2][1]:
                group_distances(group_of[sq - 2][0])
            if (sq - 1) in T_BATCHES:
                t0, t9 = T_BATCHES[sq - 1]
                batch_t(FIRST[t0], FIRST[t9])
            for t0, t9, last in Q_BATCHES:
                if sq - 1 == last:
                    normalise_and_store(FIRST[t0], FIRST[t9], nc.gpsimd if t9 <= 10 else nc.vector)
            if ok(sq):
                sum_squares(sq)
                if sq not in group_of:
                    squares_and_e(sq)
            if ok(s):
                for pr in pairs_of(s):
                    copy_x(s, pr)
            if s == 0:
                regroup_w1(0)
                nc.vector.tensor_copy(out=b1col[:], in_=b1raw[:])
                quantise_w1(0)
                regroup_w1(1)
                regroup_w1(3)

        with tc.manual_schedule(engines={mybir.EngineType.PE, mybir.EngineType.Activation, mybir.EngineType.DVE}):
            idle = bank([P, 2 * P])
            for r in range(WARM_UP):
                nc.tensor.matmul(idle[:], lhsT=zeros[:, 0:P], rhs=zeros[:], start=True, stop=True)
            for s in range(HEAD):
                step(s)
        for s in range(HEAD, NT + 5 + TRAIL + SQ_LAG):
            step(s)
